import numpy as np
import ml_dtypes


def mxq(x, axis, fmt="e4m3"):
    dtype, down = {"e4m3": (ml_dtypes.float8_e4m3fn, 7), "e5m2": (ml_dtypes.float8_e5m2, 14)}[fmt]
    v = np.moveaxis(np.asarray(x, np.float32).astype(ml_dtypes.bfloat16).astype(np.float64), axis, -1)
    blocks = v.reshape(v.shape[:-1] + (-1, 32))
    amax = np.abs(blocks).max(-1, keepdims=True)
    byte = np.maximum(np.where(amax > 0, np.frexp(amax)[1] - 1 + 127, 0) - down, 1)
    scale = np.exp2(byte - 127.0)
    codes = (blocks / scale).astype(np.float32).astype(dtype).astype(np.float64)
    return np.moveaxis((codes * scale).reshape(v.shape), -1, axis)


WIDE = False


def mx_kscale(k):
    if not WIDE:
        return np.ones(k)
    levels = np.array([10, -10, 5, -5, 0])
    a = np.random.permutation(np.resize(levels, k // 512 * 4)).reshape(k // 512, 4)
    idx = np.arange(k)
    return np.exp2(a[idx // 512, idx % 128 // 32])


BF16 = ml_dtypes.bfloat16


def bf(x):
    return np.asarray(x, np.float32).astype(BF16)


def f64(x):
    return np.asarray(x).astype(np.float64)


E2M1 = np.array([0.0, 0.5, 1.0, 1.5, 2.0, 3.0, 4.0, 6.0, -0.0, -0.5, -1.0, -1.5, -2.0, -3.0, -4.0, -6.0])


def pack_weight(w, fmt):
    k, n = w.shape
    w = f64(bf(w)).reshape(k // 32, 32, n)
    amax = np.abs(w).max(1)
    if fmt == "e4m3":
        byte = np.frexp(amax)[1] - 1 + 127 - 7
    else:
        mant, ex = np.frexp(amax / 6.0)
        byte = np.where(mant > 0.5, ex, ex - 1) + 127
    byte = np.clip(np.where(amax > 0, byte, 1), 1, 254)
    scaled = (w * np.exp2(127.0 - byte)[:, None, :]).reshape(k, n).astype(np.float32)
    by_word = np.ascontiguousarray(scaled.reshape(k // 512, 128, 4, n).transpose(0, 1, 3, 2))
    if fmt == "e4m3":
        words = by_word.astype(ml_dtypes.float8_e4m3fn).view(np.uint8)
    else:
        c = by_word.astype(ml_dtypes.float4_e2m1fn).view(np.uint8) & 0xF
        words = c[..., 0::2] | (c[..., 1::2] << 4)
    return np.ascontiguousarray(words), np.ascontiguousarray(byte.astype(np.uint8).reshape(k // 512, 16, n))


def unpack_weight(words, scales, fmt):
    g, p, n, _ = words.shape
    if fmt == "e4m3":
        vals = np.ascontiguousarray(words).view(ml_dtypes.float8_e4m3fn).astype(np.float64)
    else:
        nib = np.empty((g, p, n, 4), np.uint8)
        nib[..., 0::2] = words & 0xF
        nib[..., 1::2] = words >> 4
        vals = E2M1[nib]
    vals = vals * np.repeat(np.exp2(scales.astype(np.float64) - 127.0), 8, axis=1)[..., None]
    return vals.transpose(0, 1, 3, 2).reshape(g * 512, n)


B, I, H = 1024, 512, 512
K = H + I
FMT = "e4m3"
NAMES = ["w_f_light", "w_i_light", "w_c_light", "w_o_light",
         "w_f_light_temp", "w_i_light_temp", "w_c_light_temp", "w_o_light_temp"]


def sigmoid(v):
    return 1.0 / (1.0 + np.exp(-v))


def setup_inputs():
    s = mx_kscale(K)
    inp = {
        "y": bf(np.random.standard_normal((B, I)) * s[H:]),
        "h_light": bf(np.random.standard_normal((B, H)) * s[:H]),
        "c_light": bf(np.random.standard_normal((B, H))),
        "h_temp": bf(np.random.standard_normal((B, H)) * s[:H]),
        "c_temp": bf(np.random.standard_normal((B, H))),
    }
    for n in NAMES:
        w = np.random.standard_normal((H, K)) / np.sqrt(K) / s
        words, scales = pack_weight(np.ascontiguousarray(w.T), FMT)
        inp[n + "_words"] = words
        inp[n + "_scales"] = scales
        inp["b" + n[1:]] = bf(np.random.standard_normal(H) * 0.5)
    return inp


def _branch(hx, wf, b_f, wi, b_i, wc, b_c, wo, b_o):
    W = np.concatenate([wf, wi, wc, wo], axis=1)
    b = np.concatenate([b_f, b_i, b_c, b_o], axis=0)
    z = (mxq(hx, 1, "e4m3") @ W) + b
    zf, zi, zc, zo = np.split(z, 4, axis=1)
    return sigmoid(zf), sigmoid(zi), np.tanh(zc), sigmoid(zo)


def reference(y, h_light, c_light, h_temp, c_temp,
              w_f_light_words, w_f_light_scales, b_f_light, w_i_light_words, w_i_light_scales, b_i_light,
              w_c_light_words, w_c_light_scales, b_c_light, w_o_light_words, w_o_light_scales, b_o_light,
              w_f_light_temp_words, w_f_light_temp_scales, b_f_light_temp,
              w_i_light_temp_words, w_i_light_temp_scales, b_i_light_temp,
              w_c_light_temp_words, w_c_light_temp_scales, b_c_light_temp,
              w_o_light_temp_words, w_o_light_temp_scales, b_o_light_temp):
    y, h_light, c_light, h_temp = f64(y), f64(h_light), f64(c_light), f64(h_temp)
    hx_l = np.concatenate([h_light, y], axis=1)
    hx_t = np.concatenate([h_temp, y], axis=1)
    f1, i1, ch1, o1 = _branch(hx_l, unpack_weight(w_f_light_words, w_f_light_scales, FMT), f64(b_f_light),
                              unpack_weight(w_i_light_words, w_i_light_scales, FMT), f64(b_i_light),
                              unpack_weight(w_c_light_words, w_c_light_scales, FMT), f64(b_c_light),
                              unpack_weight(w_o_light_words, w_o_light_scales, FMT), f64(b_o_light))
    f2, i2, ch2, o2 = _branch(hx_t, unpack_weight(w_f_light_temp_words, w_f_light_temp_scales, FMT), f64(b_f_light_temp),
                              unpack_weight(w_i_light_temp_words, w_i_light_temp_scales, FMT), f64(b_i_light_temp),
                              unpack_weight(w_c_light_temp_words, w_c_light_temp_scales, FMT), f64(b_c_light_temp),
                              unpack_weight(w_o_light_temp_words, w_o_light_temp_scales, FMT), f64(b_o_light_temp))
    c_new = (f1 * c_light + i1 * ch1) + (f2 * c_light + i2 * ch2)
    h_new = (o1 + o2) * np.tanh(c_new)
    return h_new, c_new

@@ -1,0 +1,293 @@
+from contextlib import ExitStack
+
+import concourse.mybir as mybir
+from concourse.masks import make_identity
+
+F32 = mybir.dt.float32
+BF16 = mybir.dt.bfloat16
+I32 = mybir.dt.int32
+U32 = mybir.dt.uint32
+U8 = mybir.dt.uint8
+FP8X4 = mybir.dt.float8_e4m3fn_x4
+SIGMOID = mybir.ActivationFunctionType.Sigmoid
+TANH = mybir.ActivationFunctionType.Tanh
+ADD = mybir.AluOpType.add
+MULT = mybir.AluOpType.mult
+
+P = 128
+ROWS = 1024
+H = 512
+K_PASSES = 2
+F_TILES = H // P
+BANK_ROWS = 256
+
+CHUNK_ROWS = (512, 256, 256)
+
+FLOPS = 2 * ROWS * (2 * H) * (8 * H)
+BYTES = 4 * ROWS * H * 2 + 8 * (2 * H * H + 2 * 16 * H + H * 2) + 2 * ROWS * H * 4
+
+
+def tile_customlstmcell_kernel(
+    tc, y, h_light, c_light, h_temp, c_temp,
+    w_f_light_words, w_f_light_scales, b_f_light,
+    w_i_light_words, w_i_light_scales, b_i_light,
+    w_c_light_words, w_c_light_scales, b_c_light,
+    w_o_light_words, w_o_light_scales, b_o_light,
+    w_f_light_temp_words, w_f_light_temp_scales, b_f_light_temp,
+    w_i_light_temp_words, w_i_light_temp_scales, b_i_light_temp,
+    w_c_light_temp_words, w_c_light_temp_scales, b_c_light_temp,
+    w_o_light_temp_words, w_o_light_temp_scales, b_o_light_temp,
+    out_0, out_1,
+):
+    nc = tc.nc
+    h_new, c_new = out_0, out_1
+    x_dram = {"h_light": h_light, "h_temp": h_temp, "y": y}
+
+    gates = (
+        ("i1", w_i_light_words, w_i_light_scales, b_i_light, "h_light", SIGMOID),
+        ("c1", w_c_light_words, w_c_light_scales, b_c_light, "h_light", TANH),
+        ("i2", w_i_light_temp_words, w_i_light_temp_scales, b_i_light_temp, "h_temp", SIGMOID),
+        ("c2", w_c_light_temp_words, w_c_light_temp_scales, b_c_light_temp, "h_temp", TANH),
+        ("f1", w_f_light_words, w_f_light_scales, b_f_light, "h_light", SIGMOID),
+        ("f2", w_f_light_temp_words, w_f_light_temp_scales, b_f_light_temp, "h_temp", SIGMOID),
+        ("o1", w_o_light_words, w_o_light_scales, b_o_light, "h_light", SIGMOID),
+        ("o2", w_o_light_temp_words, w_o_light_temp_scales, b_o_light_temp, "h_temp", SIGMOID),
+    )
+    gate_number = {gate[0]: number for number, gate in enumerate(gates)}
+    chunk_start = [sum(CHUNK_ROWS[:j]) for j in range(len(CHUNK_ROWS))]
+    last_chunk = len(CHUNK_ROWS) - 1
+
+    with ExitStack() as ctx:
+        keep_pool = ctx.enter_context(tc.tile_pool(name="resident", bufs=1))
+        stage = ctx.enter_context(tc.tile_pool(name="stage", bufs=3))
+        acts = ctx.enter_context(tc.tile_pool(name="acts", bufs=1))
+        rowwise = ctx.enter_context(tc.tile_pool(name="rowwise", bufs=4))
+        z_banks = ctx.enter_context(tc.psum_pool(name="z_banks", bufs=4))
+        t_banks = ctx.enter_context(tc.psum_pool(name="t_banks", bufs=4))
+
+        warm = keep_pool.tile([P, 1], F32, name="warm")
+        nc.vector.memset(warm[:], 0.0)
+        nc.scalar.activation(out=warm[:], in_=warm[:], func=SIGMOID)
+
+        identity = keep_pool.tile([P, P], F32, name="identity")
+        make_identity(nc, identity[:])
+
+        w_planes = keep_pool.tile([P, len(gates) // 2, H], U8, name="w_planes", align_bytes=64)
+        nc.vector.memset(w_planes[:].bitcast(I32), 0)
+
+        bias_rows = keep_pool.tile([P, P], BF16, name="bias_rows")
+        nc.vector.memset(bias_rows[:], 0.0)
+
+        x_raw, c_rows, w_words = {}, {}, {}
+
+        def load_x(j, operand):
+            rows = x_dram[operand][chunk_start[j] : chunk_start[j] + CHUNK_ROWS[j], :]
+            raw = keep_pool.tile([P, CHUNK_ROWS[j] // P, H], BF16, name="raw_%s_%d" % (operand, j))
+            nc.sync.dma_start(out=raw[:], in_=rows.rearrange("(b p) k -> p b k", p=P))
+            x_raw[(j, operand)] = raw
+
+        def load_c(j):
+            rows = c_light[chunk_start[j] : chunk_start[j] + CHUNK_ROWS[j], :]
+            tile_c = keep_pool.tile([P, CHUNK_ROWS[j] // P, H], BF16, name="c_rows_%d" % j)
+            nc.sync.dma_start(out=tile_c[:], in_=rows.rearrange("(b p) k -> p b k", p=P))
+            c_rows[j] = tile_c
+
+        def plane_start(number, k_pass):
+            return 4 * (K_PASSES * (number % 2) + k_pass)
+
+        def load_weight(name):
+            number = gate_number[name]
+            words_dram, scales_dram = gates[number][1], gates[number][2]
+            for quadrant in range(4):
+                first = 32 * quadrant + plane_start(number, 0)
+                nc.sync.dma_start(
+                    out=w_planes[first : first + 4 * K_PASSES, number // 2, :].bitcast(I32),
+                    in_=scales_dram[:, 4 * quadrant : 4 * quadrant + 4, :].bitcast(I32),
+                )
+            words = keep_pool.tile([P, K_PASSES, H], U32, name="words_%s" % name, align_bytes=64)
+            nc.sync.dma_start(
+                out=words[:].bitcast(I32),
+                in_=words_dram.rearrange("g p n t -> p g (n t)").bitcast(I32),
+            )
+            w_words[name] = words
+
+        def load_biases():
+            for number, gate in enumerate(gates):
+                nc.sync.dma_start(
+                    out=bias_rows[F_TILES * number : F_TILES * (number + 1), :],
+                    in_=gate[3].rearrange("(f c) -> f c", c=P),
+                )
+
+        load_x(0, "h_light")
+        load_x(0, "y")
+        load_weight("i1")
+        load_biases()
+        load_weight("c1")
+        load_x(0, "h_temp")
+        load_weight("i2")
+        load_weight("c2")
+        for operand in ("h_light", "y", "h_temp"):
+            load_x(1, operand)
+        load_weight("f1")
+        load_weight("f2")
+        load_weight("o1")
+        load_c(0)
+        load_weight("o2")
+        for j in range(1, len(CHUNK_ROWS)):
+            if j + 1 <= last_chunk:
+                for operand in ("h_light", "y", "h_temp"):
+                    load_x(j + 1, operand)
+            load_c(j)
+
+        x_grouped, x_codes, x_planes = {}, {}, {}
+
+        def transpose_x(j, operand):
+            n_rows = CHUNK_ROWS[j]
+            grouped = stage.tile([P, 4 * n_rows], BF16, tag="grouped", align_bytes=64)
+            grouped_words = grouped[:].bitcast(F32).rearrange("p (r u) -> p r u", u=2)
+            for bank in range(n_rows // BANK_ROWS):
+                turned = t_banks.tile([P, 2, BANK_ROWS], F32, tag="t")
+                for half in range(BANK_ROWS // P):
+                    words = x_raw[(j, operand)][:, bank * (BANK_ROWS // P) + half, :].bitcast(F32)
+                    for u in range(2):
+                        nc.tensor.transpose(
+                            out=turned[:, u, half * P : (half + 1) * P],
+                            in_=words[:, u : H // 2 : 2],
+                            identity=identity[:],
+                        )
+                copy_out = nc.vector.tensor_copy if bank % 2 == 0 else nc.scalar.copy
+                copy_out(
+                    out=grouped_words[:, bank * BANK_ROWS : (bank + 1) * BANK_ROWS, :],
+                    in_=turned[:].rearrange("p u r -> p r u"),
+                )
+            x_grouped[(j, operand)] = grouped
+
+        def quantise_x(j, operand):
+            n_rows = CHUNK_ROWS[j]
+            codes = keep_pool.tile([P, n_rows], U32, name="codes_%s_%d" % (operand, j), align_bytes=64)
+            plane = keep_pool.tile([P, n_rows], U8, name="plane_%s_%d" % (operand, j), align_bytes=64)
+            nc.vector.quantize_mx(
+                out=codes[:].bitcast(FP8X4), scales=plane[:], in_=x_grouped[(j, operand)][:]
+            )
+            x_codes[(j, operand)], x_planes[(j, operand)] = codes, plane
+
+        bias_cols = keep_pool.tile([P, P], F32, name="bias_cols")
+
+        def transpose_biases():
+            bias_f32 = keep_pool.tile([P, P], F32, name="bias_f32")
+            nc.gpsimd.tensor_copy(out=bias_f32[:], in_=bias_rows[:])
+            turned = t_banks.tile([P, P], F32, tag="t")
+            nc.tensor.transpose(out=turned[:], in_=bias_f32[:], identity=identity[:])
+            nc.scalar.copy(out=bias_cols[:], in_=turned[:])
+
+        def gate(j, name, bufs=1):
+            number = gate_number[name]
+            hidden, func = gates[number][4], gates[number][5]
+            result = acts.tile([P, F_TILES, CHUNK_ROWS[j]], F32, tag=name, name="act_" + name, bufs=bufs)
+            for f in range(F_TILES):
+                cols = slice(f * P, (f + 1) * P)
+                z = z_banks.tile([P, CHUNK_ROWS[j]], F32, tag="z")
+                for k_pass, operand in enumerate((hidden, "y")):
+                    nc.tensor.matmul_mx(
+                        out=z[:],
+                        lhsT=w_words[name][:, k_pass, cols].bitcast(FP8X4),
+                        lhsT_scale=w_planes[plane_start(number, k_pass) : P, number // 2, cols],
+                        rhs=x_codes[(j, operand)][:].bitcast(FP8X4),
+                        rhs_scale=x_planes[(j, operand)][:],
+                        start=(k_pass == 0),
+                        stop=(k_pass == K_PASSES - 1),
+                    )
+                column = F_TILES * number + f
+                nc.scalar.activation(
+                    out=result[:, f, :], in_=z[:], func=func, bias=bias_cols[:, column : column + 1]
+                )
+            return result
+
+        def combine(target, other, op):
+            for f in range(F_TILES):
+                nc.vector.tensor_tensor(out=target[:, f, :], in0=target[:, f, :], in1=other[:, f, :], op=op)
+
+        def turn_back(source, block):
+            bank = t_banks.tile([P, H], F32, tag="t")
+            for f in range(F_TILES):
+                nc.tensor.transpose(
+                    out=bank[:, f * P : (f + 1) * P],
+                    in_=source[:, f, block * P : (block + 1) * P],
+                    identity=identity[:],
+                )
+            return bank
+
+        def out_rows(dram, j, block):
+            first = chunk_start[j] + block * P
+            return dram[first : first + P, :]
+
+        def cell_state(j, keep, feed, blocks, c_tiles):
+            banks = [(turn_back(keep, block), turn_back(feed, block)) for block in blocks]
+            for block, (keep_bank, feed_bank) in zip(blocks, banks):
+                kept = rowwise.tile([P, H], F32, tag="kept", bufs=2)
+                nc.vector.tensor_tensor(out=kept[:], in0=keep_bank[:], in1=c_rows[j][:, block, :], op=MULT)
+                c_tile = rowwise.tile([P, H], F32, tag="c_new")
+                nc.vector.tensor_tensor(out=c_tile[:], in0=feed_bank[:], in1=kept[:], op=ADD)
+                nc.sync.dma_start(out=out_rows(c_new, j, block), in_=c_tile[:])
+                c_tiles[block] = c_tile
+
+        def tanh_of_cell(blocks, c_tiles, tanh_c):
+            for block in blocks:
+                nc.scalar.activation(out=tanh_c[:, block, :], in_=c_tiles[block][:], func=TANH)
+
+        def hidden_state(j, open_gate, tanh_c):
+            blocks = range(CHUNK_ROWS[j] // P)
+            banks = [turn_back(open_gate, block) for block in blocks]
+            for block in blocks:
+                h_tile = rowwise.tile([P, H], F32, tag="h_new")
+                nc.vector.tensor_tensor(out=h_tile[:], in0=banks[block][:], in1=tanh_c[:, block, :], op=MULT)
+                nc.sync.dma_start(out=out_rows(h_new, j, block), in_=h_tile[:])
+
+        def finish_chunk(j, open_gate, late, c_tiles, tanh_c):
+            tanh_of_cell(late, c_tiles, tanh_c)
+            hidden_state(j, open_gate, tanh_c)
+
+        transpose_x(0, "h_light")
+        transpose_x(0, "y")
+        quantise_x(0, "h_light")
+        quantise_x(0, "y")
+        transpose_biases()
+
+        for j in range(len(CHUNK_ROWS)):
+            n_blocks = CHUNK_ROWS[j] // P
+            early, late = range(n_blocks // 2), range(n_blocks // 2, n_blocks)
+
+            feed = gate(j, "i1", bufs=2)
+            if j == 0:
+                transpose_x(0, "h_temp")
+                quantise_x(0, "h_temp")
+            else:
+                finish_chunk(*unfinished)
+            candidate = gate(j, "c1")
+            combine(feed, candidate, MULT)
+
+            feed_2 = gate(j, "i2")
+            if j < last_chunk:
+                transpose_x(j + 1, "h_light")
+                transpose_x(j + 1, "y")
+            candidate = gate(j, "c2")
+            combine(feed_2, candidate, MULT)
+            combine(feed, feed_2, ADD)
+            if j < last_chunk:
+                transpose_x(j + 1, "h_temp")
+                for operand in ("h_light", "y", "h_temp"):
+                    quantise_x(j + 1, operand)
+
+            keep = gate(j, "f1", bufs=2)
+            combine(keep, gate(j, "f2"), ADD)
+
+            open_gate = gate(j, "o1", bufs=2)
+            c_tiles = {}
+            tanh_c = rowwise.tile([P, n_blocks, H], F32, tag="tanh_c", bufs=2)
+            cell_state(j, keep, feed, early, c_tiles)
+            combine(open_gate, gate(j, "o2"), ADD)
+            tanh_of_cell(early, c_tiles, tanh_c)
+            cell_state(j, keep, feed, late, c_tiles)
+            unfinished = (j, open_gate, late, c_tiles, tanh_c)
+
+        finish_chunk(*unfinished)

@@ -64,6 +64,7 @@ def tile_customlstmcell_kernel(
         rowwise = ctx.enter_context(tc.tile_pool(name="rowwise", bufs=4))
         z_banks = ctx.enter_context(tc.psum_pool(name="z_banks", bufs=4))
         t_banks = ctx.enter_context(tc.psum_pool(name="t_banks", bufs=4))
+        ctx.enter_context(tc.manual_schedule())
 
         warm = keep_pool.tile([P, 1], F32, name="warm")
         nc.vector.memset(warm[:], 0.0)

@@ -19,9 +19,12 @@ ROWS = 1024
 H = 512
 K_PASSES = 2
 F_TILES = H // P
-BANK_ROWS = 256
-
-CHUNK_ROWS = (512, 256, 256)
+CHUNK = 512
+N_CHUNKS = ROWS // CHUNK
+BLOCKS = CHUNK // P
+EARLY, LATE = (0, 1), (2, 3)
+BANK = 512
+BANK_ROWS = BANK // 2
 
 FLOPS = 2 * ROWS * (2 * H) * (8 * H)
 BYTES = 4 * ROWS * H * 2 + 8 * (2 * H * H + 2 * 16 * H + H * 2) + 2 * ROWS * H * 4
@@ -54,11 +57,9 @@ def tile_customlstmcell_kernel(
         ("o2", w_o_light_temp_words, w_o_light_temp_scales, b_o_light_temp, "h_temp", SIGMOID),
     )
     gate_number = {gate[0]: number for number, gate in enumerate(gates)}
-    chunk_start = [sum(CHUNK_ROWS[:j]) for j in range(len(CHUNK_ROWS))]
-    last_chunk = len(CHUNK_ROWS) - 1
 
     with ExitStack() as ctx:
-        keep_pool = ctx.enter_context(tc.tile_pool(name="resident", bufs=1))
+        resident = ctx.enter_context(tc.tile_pool(name="resident", bufs=1))
         stage = ctx.enter_context(tc.tile_pool(name="stage", bufs=3))
         acts = ctx.enter_context(tc.tile_pool(name="acts", bufs=1))
         rowwise = ctx.enter_context(tc.tile_pool(name="rowwise", bufs=4))
@@ -66,46 +67,44 @@ def tile_customlstmcell_kernel(
         t_banks = ctx.enter_context(tc.psum_pool(name="t_banks", bufs=4))
         ctx.enter_context(tc.manual_schedule())
 
-        warm = keep_pool.tile([P, 1], F32, name="warm")
+        warm = resident.tile([P, 1], F32, name="warm")
         nc.vector.memset(warm[:], 0.0)
         nc.scalar.activation(out=warm[:], in_=warm[:], func=SIGMOID)
 
-        identity = keep_pool.tile([P, P], F32, name="identity")
+        identity = resident.tile([P, P], F32, name="identity")
         make_identity(nc, identity[:])
 
-        w_planes = keep_pool.tile([P, len(gates) // 2, H], U8, name="w_planes", align_bytes=64)
+        w_planes = resident.tile([P, len(gates), H], U8, name="w_planes", align_bytes=64)
         nc.vector.memset(w_planes[:].bitcast(I32), 0)
 
-        bias_rows = keep_pool.tile([P, P], BF16, name="bias_rows")
+        bias_rows = resident.tile([P, P], BF16, name="bias_rows")
         nc.vector.memset(bias_rows[:], 0.0)
 
         x_raw, c_rows, w_words = {}, {}, {}
 
+        def load_rows(dram, j, name):
+            rows = resident.tile([P, BLOCKS, H], BF16, name="%s_%d" % (name, j))
+            nc.sync.dma_start(
+                out=rows[:], in_=dram[j * CHUNK : (j + 1) * CHUNK, :].rearrange("(b p) k -> p b k", p=P)
+            )
+            return rows
+
         def load_x(j, operand):
-            rows = x_dram[operand][chunk_start[j] : chunk_start[j] + CHUNK_ROWS[j], :]
-            raw = keep_pool.tile([P, CHUNK_ROWS[j] // P, H], BF16, name="raw_%s_%d" % (operand, j))
-            nc.sync.dma_start(out=raw[:], in_=rows.rearrange("(b p) k -> p b k", p=P))
-            x_raw[(j, operand)] = raw
+            x_raw[(j, operand)] = load_rows(x_dram[operand], j, operand)
 
         def load_c(j):
-            rows = c_light[chunk_start[j] : chunk_start[j] + CHUNK_ROWS[j], :]
-            tile_c = keep_pool.tile([P, CHUNK_ROWS[j] // P, H], BF16, name="c_rows_%d" % j)
-            nc.sync.dma_start(out=tile_c[:], in_=rows.rearrange("(b p) k -> p b k", p=P))
-            c_rows[j] = tile_c
-
-        def plane_start(number, k_pass):
-            return 4 * (K_PASSES * (number % 2) + k_pass)
+            c_rows[j] = load_rows(c_light, j, "c_light")
 
         def load_weight(name):
             number = gate_number[name]
             words_dram, scales_dram = gates[number][1], gates[number][2]
             for quadrant in range(4):
-                first = 32 * quadrant + plane_start(number, 0)
+                first = 32 * quadrant
                 nc.sync.dma_start(
-                    out=w_planes[first : first + 4 * K_PASSES, number // 2, :].bitcast(I32),
+                    out=w_planes[first : first + 4 * K_PASSES, number, :].bitcast(I32),
                     in_=scales_dram[:, 4 * quadrant : 4 * quadrant + 4, :].bitcast(I32),
                 )
-            words = keep_pool.tile([P, K_PASSES, H], U32, name="words_%s" % name, align_bytes=64)
+            words = resident.tile([P, K_PASSES, H], U32, name="words_%s" % name, align_bytes=64)
             nc.sync.dma_start(
                 out=words[:].bitcast(I32),
                 in_=words_dram.rearrange("g p n t -> p g (n t)").bitcast(I32),
@@ -126,27 +125,22 @@ def tile_customlstmcell_kernel(
         load_weight("c1")
         load_x(0, "h_temp")
         load_weight("i2")
-        load_weight("c2")
         for operand in ("h_light", "y", "h_temp"):
             load_x(1, operand)
+        load_weight("c2")
         load_weight("f1")
         load_weight("f2")
         load_weight("o1")
         load_c(0)
         load_weight("o2")
-        for j in range(1, len(CHUNK_ROWS)):
-            if j + 1 <= last_chunk:
-                for operand in ("h_light", "y", "h_temp"):
-                    load_x(j + 1, operand)
-            load_c(j)
+        load_c(1)
 
         x_grouped, x_codes, x_planes = {}, {}, {}
 
         def transpose_x(j, operand):
-            n_rows = CHUNK_ROWS[j]
-            grouped = stage.tile([P, 4 * n_rows], BF16, tag="grouped", align_bytes=64)
+            grouped = stage.tile([P, 4 * CHUNK], BF16, tag="grouped", align_bytes=64)
             grouped_words = grouped[:].bitcast(F32).rearrange("p (r u) -> p r u", u=2)
-            for bank in range(n_rows // BANK_ROWS):
+            for bank in range(CHUNK // BANK_ROWS):
                 turned = t_banks.tile([P, 2, BANK_ROWS], F32, tag="t")
                 for half in range(BANK_ROWS // P):
                     words = x_raw[(j, operand)][:, bank * (BANK_ROWS // P) + half, :].bitcast(F32)
@@ -164,45 +158,54 @@ def tile_customlstmcell_kernel(
             x_grouped[(j, operand)] = grouped
 
         def quantise_x(j, operand):
-            n_rows = CHUNK_ROWS[j]
-            codes = keep_pool.tile([P, n_rows], U32, name="codes_%s_%d" % (operand, j), align_bytes=64)
-            plane = keep_pool.tile([P, n_rows], U8, name="plane_%s_%d" % (operand, j), align_bytes=64)
+            codes = resident.tile([P, CHUNK], U32, name="codes_%s_%d" % (operand, j), align_bytes=64)
+            plane = resident.tile([P, CHUNK], U8, name="plane_%s_%d" % (operand, j), align_bytes=64)
             nc.vector.quantize_mx(
                 out=codes[:].bitcast(FP8X4), scales=plane[:], in_=x_grouped[(j, operand)][:]
             )
             x_codes[(j, operand)], x_planes[(j, operand)] = codes, plane
 
-        bias_cols = keep_pool.tile([P, P], F32, name="bias_cols")
+        bias_cols = resident.tile([P, P], F32, name="bias_cols")
 
         def transpose_biases():
-            bias_f32 = keep_pool.tile([P, P], F32, name="bias_f32")
+            bias_f32 = resident.tile([P, P], F32, name="bias_f32")
             nc.gpsimd.tensor_copy(out=bias_f32[:], in_=bias_rows[:])
             turned = t_banks.tile([P, P], F32, tag="t")
             nc.tensor.transpose(out=turned[:], in_=bias_f32[:], identity=identity[:])
             nc.scalar.copy(out=bias_cols[:], in_=turned[:])
 
-        def gate(j, name, bufs=1):
+        def multiply(j, name):
             number = gate_number[name]
-            hidden, func = gates[number][4], gates[number][5]
-            result = acts.tile([P, F_TILES, CHUNK_ROWS[j]], F32, tag=name, name="act_" + name, bufs=bufs)
+            banks = []
             for f in range(F_TILES):
                 cols = slice(f * P, (f + 1) * P)
-                z = z_banks.tile([P, CHUNK_ROWS[j]], F32, tag="z")
-                for k_pass, operand in enumerate((hidden, "y")):
+                z = z_banks.tile([P, CHUNK], F32, tag="z")
+                for k_pass, operand in enumerate((gates[number][4], "y")):
                     nc.tensor.matmul_mx(
                         out=z[:],
                         lhsT=w_words[name][:, k_pass, cols].bitcast(FP8X4),
-                        lhsT_scale=w_planes[plane_start(number, k_pass) : P, number // 2, cols],
+                        lhsT_scale=w_planes[4 * k_pass : P, number, cols],
                         rhs=x_codes[(j, operand)][:].bitcast(FP8X4),
                         rhs_scale=x_planes[(j, operand)][:],
                         start=(k_pass == 0),
                         stop=(k_pass == K_PASSES - 1),
                     )
+                banks.append(z)
+            return banks
+
+        def activate(name, banks, bufs=1):
+            number = gate_number[name]
+            result = acts.tile([P, F_TILES, CHUNK], F32, tag=name, name="act_" + name, bufs=bufs)
+            for f in range(F_TILES):
                 column = F_TILES * number + f
                 nc.scalar.activation(
-                    out=result[:, f, :], in_=z[:], func=func, bias=bias_cols[:, column : column + 1]
+                    out=result[:, f, :], in_=banks[f][:], func=gates[number][5],
+                    bias=bias_cols[:, column : column + 1],
                 )
             return result
+
+        def gate(j, name, bufs=1):
+            return activate(name, multiply(j, name), bufs)
 
         def combine(target, other, op):
             for f in range(F_TILES):
@@ -219,7 +222,7 @@ def tile_customlstmcell_kernel(
             return bank
 
         def out_rows(dram, j, block):
-            first = chunk_start[j] + block * P
+            first = j * CHUNK + block * P
             return dram[first : first + P, :]
 
         def cell_state(j, keep, feed, blocks, c_tiles):
@@ -232,63 +235,61 @@ def tile_customlstmcell_kernel(
                 nc.sync.dma_start(out=out_rows(c_new, j, block), in_=c_tile[:])
                 c_tiles[block] = c_tile
 
-        def tanh_of_cell(blocks, c_tiles, tanh_c):
+        def tanh_of_cell(blocks, c_tiles, tanh_tiles):
             for block in blocks:
-                nc.scalar.activation(out=tanh_c[:, block, :], in_=c_tiles[block][:], func=TANH)
+                tanh_c = rowwise.tile([P, H], F32, tag="tanh_c")
+                nc.scalar.activation(out=tanh_c[:], in_=c_tiles[block][:], func=TANH)
+                tanh_tiles[block] = tanh_c
 
-        def hidden_state(j, open_gate, tanh_c):
-            blocks = range(CHUNK_ROWS[j] // P)
-            banks = [turn_back(open_gate, block) for block in blocks]
-            for block in blocks:
+        def hidden_state(j, open_gate, tanh_tiles):
+            banks = [turn_back(open_gate, block) for block in range(BLOCKS)]
+            for block in range(BLOCKS):
                 h_tile = rowwise.tile([P, H], F32, tag="h_new")
-                nc.vector.tensor_tensor(out=h_tile[:], in0=banks[block][:], in1=tanh_c[:, block, :], op=MULT)
+                nc.vector.tensor_tensor(out=h_tile[:], in0=banks[block][:], in1=tanh_tiles[block][:], op=MULT)
                 nc.sync.dma_start(out=out_rows(h_new, j, block), in_=h_tile[:])
 
-        def finish_chunk(j, open_gate, late, c_tiles, tanh_c):
-            tanh_of_cell(late, c_tiles, tanh_c)
-            hidden_state(j, open_gate, tanh_c)
+        def finish_chunk(j, open_gate, c_tiles, tanh_tiles):
+            tanh_of_cell(LATE, c_tiles, tanh_tiles)
+            hidden_state(j, open_gate, tanh_tiles)
 
         transpose_x(0, "h_light")
         transpose_x(0, "y")
         quantise_x(0, "h_light")
         quantise_x(0, "y")
-        transpose_biases()
 
-        for j in range(len(CHUNK_ROWS)):
-            n_blocks = CHUNK_ROWS[j] // P
-            early, late = range(n_blocks // 2), range(n_blocks // 2, n_blocks)
-
-            feed = gate(j, "i1", bufs=2)
+        for j in range(N_CHUNKS):
+            banks = multiply(j, "i1")
+            if j == 0:
+                transpose_biases()
+            feed = activate("i1", banks, bufs=2)
             if j == 0:
                 transpose_x(0, "h_temp")
                 quantise_x(0, "h_temp")
+            combine(feed, gate(j, "c1"), MULT)
+            if j == 0:
+                transpose_x(1, "h_light")
+                transpose_x(1, "y")
+                quantise_x(1, "h_light")
+                quantise_x(1, "y")
             else:
                 finish_chunk(*unfinished)
-            candidate = gate(j, "c1")
-            combine(feed, candidate, MULT)
 
             feed_2 = gate(j, "i2")
-            if j < last_chunk:
-                transpose_x(j + 1, "h_light")
-                transpose_x(j + 1, "y")
-            candidate = gate(j, "c2")
-            combine(feed_2, candidate, MULT)
+            if j == 0:
+                transpose_x(1, "h_temp")
+                quantise_x(1, "h_temp")
+            combine(feed_2, gate(j, "c2"), MULT)
             combine(feed, feed_2, ADD)
-            if j < last_chunk:
-                transpose_x(j + 1, "h_temp")
-                for operand in ("h_light", "y", "h_temp"):
-                    quantise_x(j + 1, operand)
 
             keep = gate(j, "f1", bufs=2)
             combine(keep, gate(j, "f2"), ADD)
 
             open_gate = gate(j, "o1", bufs=2)
-            c_tiles = {}
-            tanh_c = rowwise.tile([P, n_blocks, H], F32, tag="tanh_c", bufs=2)
-            cell_state(j, keep, feed, early, c_tiles)
+            c_tiles, tanh_tiles = {}, {}
+            cell_state(j, keep, feed, EARLY, c_tiles)
             combine(open_gate, gate(j, "o2"), ADD)
-            tanh_of_cell(early, c_tiles, tanh_c)
-            cell_state(j, keep, feed, late, c_tiles)
-            unfinished = (j, open_gate, late, c_tiles, tanh_c)
+            tanh_of_cell(EARLY, c_tiles, tanh_tiles)
+            cell_state(j, keep, feed, LATE, c_tiles)
+            unfinished = (j, open_gate, c_tiles, tanh_tiles)
 
         finish_chunk(*unfinished)

@@ -113,24 +113,23 @@ def tile_customlstmcell_kernel(
 
         def load_biases():
             for number, gate in enumerate(gates):
-                nc.sync.dma_start(
+                nc.gpsimd.dma_start(
                     out=bias_rows[F_TILES * number : F_TILES * (number + 1), :],
                     in_=gate[3].rearrange("(f c) -> f c", c=P),
                 )
 
+        load_biases()
         load_x(0, "h_light")
         load_x(0, "y")
         load_weight("i1")
-        load_biases()
-        load_weight("c1")
         load_x(0, "h_temp")
+        load_weight("c1")
+        load_x(1, "h_light")
+        load_x(1, "y")
         load_weight("i2")
-        for operand in ("h_light", "y", "h_temp"):
-            load_x(1, operand)
-        load_weight("c2")
-        load_weight("f1")
-        load_weight("f2")
-        load_weight("o1")
+        load_x(1, "h_temp")
+        for name in ("c2", "f1", "f2", "o1"):
+            load_weight(name)
         load_c(0)
         load_weight("o2")
         load_c(1)

@@ -113,23 +113,24 @@ def tile_customlstmcell_kernel(
 
         def load_biases():
             for number, gate in enumerate(gates):
-                nc.gpsimd.dma_start(
+                nc.sync.dma_start(
                     out=bias_rows[F_TILES * number : F_TILES * (number + 1), :],
                     in_=gate[3].rearrange("(f c) -> f c", c=P),
                 )
 
-        load_biases()
         load_x(0, "h_light")
         load_x(0, "y")
         load_weight("i1")
-        load_x(0, "h_temp")
+        load_biases()
         load_weight("c1")
-        load_x(1, "h_light")
-        load_x(1, "y")
+        load_x(0, "h_temp")
         load_weight("i2")
-        load_x(1, "h_temp")
-        for name in ("c2", "f1", "f2", "o1"):
-            load_weight(name)
+        for operand in ("h_light", "y", "h_temp"):
+            load_x(1, operand)
+        load_weight("c2")
+        load_weight("f1")
+        load_weight("f2")
+        load_weight("o1")
         load_c(0)
         load_weight("o2")
         load_c(1)
@@ -225,12 +226,17 @@ def tile_customlstmcell_kernel(
             return dram[first : first + P, :]
 
         def cell_state(j, keep, feed, blocks, c_tiles):
-            banks = [(turn_back(keep, block), turn_back(feed, block)) for block in blocks]
-            for block, (keep_bank, feed_bank) in zip(blocks, banks):
-                kept = rowwise.tile([P, H], F32, tag="kept", bufs=2)
-                nc.vector.tensor_tensor(out=kept[:], in0=keep_bank[:], in1=c_rows[j][:, block, :], op=MULT)
+            keep_banks = {block: turn_back(keep, block) for block in blocks}
+            feed_banks = {block: turn_back(feed, block) for block in blocks}
+            kept = {}
+            for block in blocks:
+                kept[block] = rowwise.tile([P, H], F32, tag="kept", name="kept", bufs=2)
+                nc.vector.tensor_tensor(
+                    out=kept[block][:], in0=keep_banks[block][:], in1=c_rows[j][:, block, :], op=MULT
+                )
+            for block in blocks:
                 c_tile = rowwise.tile([P, H], F32, tag="c_new")
-                nc.vector.tensor_tensor(out=c_tile[:], in0=feed_bank[:], in1=kept[:], op=ADD)
+                nc.vector.tensor_tensor(out=c_tile[:], in0=feed_banks[block][:], in1=kept[block][:], op=ADD)
                 nc.sync.dma_start(out=out_rows(c_new, j, block), in_=c_tile[:])
                 c_tiles[block] = c_tile
 

@@ -26,6 +26,19 @@ EARLY, LATE = (0, 1), (2, 3)
 BANK = 512
 BANK_ROWS = BANK // 2
 
+OPT = {
+    "x0_pieces": 2,
+    "split_w_i1": True,
+    "pass_major_first": True,
+    "early_biases": 4,
+    "loads": "h_temp0 c1 h_light1 i2 y1 c2 bias h_temp1 f1 f2 o1 c_light0 o2 c_light1",
+    "prep": {"c1": ("h_light",), "i2": ("y",), "c2": ("h_temp", "bias")},
+    "sorted": {},
+    "dummies": 0,
+    "open_on_pe": (),
+    "wide": {"mult": 1, "feed": 1, "keep": 1, "open": 1},
+}
+
 FLOPS = 2 * ROWS * (2 * H) * (8 * H)
 BYTES = 4 * ROWS * H * 2 + 8 * (2 * H * H + 2 * 16 * H + H * 2) + 2 * ROWS * H * 4
 
@@ -67,6 +80,27 @@ def tile_customlstmcell_kernel(
         t_banks = ctx.enter_context(tc.psum_pool(name="t_banks", bufs=4))
         ctx.enter_context(tc.manual_schedule())
 
+        bias_groups = (range(0, OPT["early_biases"]), range(OPT["early_biases"], len(gates)))
+        bias_rows = [resident.tile([P, P], BF16, name="bias_rows_%d" % group) for group in range(2)]
+        for group in range(2):
+            nc.vector.memset(bias_rows[group][:], 0.0)
+
+        def load_biases(group, queue):
+            for number in bias_groups[group]:
+                queue.dma_start(
+                    out=bias_rows[group][F_TILES * number : F_TILES * (number + 1), :],
+                    in_=gates[number][3].rearrange("(f c) -> f c", c=P),
+                )
+
+        load_biases(0, nc.scalar)
+
+        if OPT["dummies"]:
+            zeros = resident.tile([P, CHUNK], BF16, name="zeros")
+            nc.vector.memset(zeros[:], 0.0)
+            idle_bank = z_banks.tile([P, CHUNK], F32, tag="z", name="idle_bank")
+            for number in range(OPT["dummies"]):
+                nc.tensor.matmul(out=idle_bank[:], lhsT=zeros[:, 0:P], rhs=zeros[:], start=True, stop=True)
+
         warm = resident.tile([P, 1], F32, name="warm")
         nc.vector.memset(warm[:], 0.0)
         nc.scalar.activation(out=warm[:], in_=warm[:], func=SIGMOID)
@@ -77,85 +111,104 @@ def tile_customlstmcell_kernel(
         w_planes = resident.tile([P, len(gates), H], U8, name="w_planes", align_bytes=64)
         nc.vector.memset(w_planes[:].bitcast(I32), 0)
 
-        bias_rows = resident.tile([P, P], BF16, name="bias_rows")
-        nc.vector.memset(bias_rows[:], 0.0)
-
         x_raw, c_rows, w_words = {}, {}, {}
 
-        def load_rows(dram, j, name):
+        def load_rows(dram, j, name, pieces=1):
             rows = resident.tile([P, BLOCKS, H], BF16, name="%s_%d" % (name, j))
-            nc.sync.dma_start(
-                out=rows[:], in_=dram[j * CHUNK : (j + 1) * CHUNK, :].rearrange("(b p) k -> p b k", p=P)
-            )
+            per = BLOCKS // pieces
+            for piece in range(pieces):
+                first = j * CHUNK + piece * per * P
+                nc.sync.dma_start(
+                    out=rows[:, piece * per : (piece + 1) * per, :],
+                    in_=dram[first : first + per * P, :].rearrange("(b p) k -> p b k", p=P),
+                )
             return rows
 
-        def load_x(j, operand):
-            x_raw[(j, operand)] = load_rows(x_dram[operand], j, operand)
+        def load_x(j, operand, pieces=1):
+            x_raw[(j, operand)] = load_rows(x_dram[operand], j, operand, pieces)
 
         def load_c(j):
             c_rows[j] = load_rows(c_light, j, "c_light")
 
-        def load_weight(name):
+        def load_scales(name):
             number = gate_number[name]
-            words_dram, scales_dram = gates[number][1], gates[number][2]
+            scales_dram = gates[number][2]
             for quadrant in range(4):
                 first = 32 * quadrant
                 nc.sync.dma_start(
                     out=w_planes[first : first + 4 * K_PASSES, number, :].bitcast(I32),
                     in_=scales_dram[:, 4 * quadrant : 4 * quadrant + 4, :].bitcast(I32),
                 )
-            words = resident.tile([P, K_PASSES, H], U32, name="words_%s" % name, align_bytes=64)
-            nc.sync.dma_start(
-                out=words[:].bitcast(I32),
-                in_=words_dram.rearrange("g p n t -> p g (n t)").bitcast(I32),
-            )
-            w_words[name] = words
 
-        def load_biases():
-            for number, gate in enumerate(gates):
+        def load_words(name, k_pass=None):
+            words_dram = gates[gate_number[name]][1]
+            if name not in w_words:
+                w_words[name] = resident.tile([P, K_PASSES, H], U32, name="words_%s" % name, align_bytes=64)
+            words = w_words[name]
+            if k_pass is None:
                 nc.sync.dma_start(
-                    out=bias_rows[F_TILES * number : F_TILES * (number + 1), :],
-                    in_=gate[3].rearrange("(f c) -> f c", c=P),
+                    out=words[:].bitcast(I32),
+                    in_=words_dram.rearrange("g p n t -> p g (n t)").bitcast(I32),
+                )
+            else:
+                nc.sync.dma_start(
+                    out=words[:, k_pass, :].bitcast(I32),
+                    in_=words_dram[k_pass].rearrange("p n t -> p (n t)").bitcast(I32),
                 )
 
-        load_x(0, "h_light")
-        load_x(0, "y")
-        load_weight("i1")
-        load_biases()
-        load_weight("c1")
-        load_x(0, "h_temp")
-        load_weight("i2")
-        for operand in ("h_light", "y", "h_temp"):
-            load_x(1, operand)
-        load_weight("c2")
-        load_weight("f1")
-        load_weight("f2")
-        load_weight("o1")
-        load_c(0)
-        load_weight("o2")
-        load_c(1)
+        def load_weight(name):
+            load_scales(name)
+            load_words(name)
 
-        x_grouped, x_codes, x_planes = {}, {}, {}
+        load_x(0, "h_light", OPT["x0_pieces"])
+        load_x(0, "y", OPT["x0_pieces"])
+        load_scales("i1")
+        if OPT["split_w_i1"]:
+            load_words("i1", 0)
+            load_words("i1", 1)
+        else:
+            load_words("i1")
+        for token in OPT["loads"].split():
+            if token in gate_number:
+                load_weight(token)
+            elif token == "bias":
+                load_biases(1, nc.sync)
+            elif token.startswith("c_light"):
+                load_c(int(token[-1]))
+            else:
+                load_x(int(token[-1]), token[:-1])
 
-        def transpose_x(j, operand):
+        x_grouped, x_codes, x_planes, x_sorted = {}, {}, {}, {}
+
+        def transpose_x(j, operand, engines=(nc.vector, nc.scalar)):
             grouped = stage.tile([P, 4 * CHUNK], BF16, tag="grouped", align_bytes=64)
             grouped_words = grouped[:].bitcast(F32).rearrange("p (r u) -> p r u", u=2)
             for bank in range(CHUNK // BANK_ROWS):
                 turned = t_banks.tile([P, 2, BANK_ROWS], F32, tag="t")
                 for half in range(BANK_ROWS // P):
-                    words = x_raw[(j, operand)][:, bank * (BANK_ROWS // P) + half, :].bitcast(F32)
+                    block = bank * (BANK_ROWS // P) + half
+                    words = x_raw[(j, operand)][:, block, :].bitcast(F32)
                     for u in range(2):
                         nc.tensor.transpose(
                             out=turned[:, u, half * P : (half + 1) * P],
-                            in_=words[:, u : H // 2 : 2],
+                            in_=x_sorted[(j, operand)][:, block, u, :] if (j, operand) in x_sorted else words[:, u : H // 2 : 2],
                             identity=identity[:],
                         )
-                copy_out = nc.vector.tensor_copy if bank % 2 == 0 else nc.scalar.copy
+                copy_out = engines[bank].tensor_copy if engines[bank] is nc.vector else engines[bank].copy
                 copy_out(
                     out=grouped_words[:, bank * BANK_ROWS : (bank + 1) * BANK_ROWS, :],
                     in_=turned[:].rearrange("p u r -> p r u"),
                 )
             x_grouped[(j, operand)] = grouped
+
+        def sort_x(j, operand):
+            if (j, operand) in OPT["sorted"]:
+                engine = {"gpsimd": nc.gpsimd, "vector": nc.vector}[OPT["sorted"][(j, operand)]]
+                ordered = stage.tile([P, BLOCKS, 2, P], F32, tag="ordered", name="ordered")
+                engine.tensor_copy(
+                    out=ordered[:], in_=x_raw[(j, operand)][:].bitcast(F32).rearrange("p b (w u) -> p b u w", u=2)
+                )
+                x_sorted[(j, operand)] = ordered
 
         def quantise_x(j, operand):
             codes = resident.tile([P, CHUNK], U32, name="codes_%s_%d" % (operand, j), align_bytes=64)
@@ -167,30 +220,34 @@ def tile_customlstmcell_kernel(
 
         bias_cols = resident.tile([P, P], F32, name="bias_cols")
 
-        def transpose_biases():
-            bias_f32 = resident.tile([P, P], F32, name="bias_f32")
-            nc.gpsimd.tensor_copy(out=bias_f32[:], in_=bias_rows[:])
-            turned = t_banks.tile([P, P], F32, tag="t")
+        def transpose_biases(group):
+            bias_f32 = resident.tile([P, P], F32, name="bias_f32_%d" % group)
+            nc.gpsimd.tensor_copy(out=bias_f32[:], in_=bias_rows[group][:])
+            turned = t_banks.tile([P, P], F32, tag="t", name="turned_bias")
             nc.tensor.transpose(out=turned[:], in_=bias_f32[:], identity=identity[:])
-            nc.scalar.copy(out=bias_cols[:], in_=turned[:])
+            cols = slice(F_TILES * bias_groups[group].start, F_TILES * bias_groups[group].stop)
+            nc.scalar.copy(out=bias_cols[:, cols], in_=turned[:, cols])
 
-        def multiply(j, name):
+        def multiply(j, name, pass_major=False):
             number = gate_number[name]
-            banks = []
-            for f in range(F_TILES):
+            banks = [z_banks.tile([P, CHUNK], F32, tag="z", name="z") for f in range(F_TILES)]
+            operands = (gates[number][4], "y")
+            if pass_major:
+                order = [(f, k_pass) for k_pass in range(K_PASSES) for f in range(F_TILES)]
+            else:
+                order = [(f, k_pass) for f in range(F_TILES) for k_pass in range(K_PASSES)]
+            for f, k_pass in order:
                 cols = slice(f * P, (f + 1) * P)
-                z = z_banks.tile([P, CHUNK], F32, tag="z")
-                for k_pass, operand in enumerate((gates[number][4], "y")):
-                    nc.tensor.matmul_mx(
-                        out=z[:],
-                        lhsT=w_words[name][:, k_pass, cols].bitcast(FP8X4),
-                        lhsT_scale=w_planes[4 * k_pass : P, number, cols],
-                        rhs=x_codes[(j, operand)][:].bitcast(FP8X4),
-                        rhs_scale=x_planes[(j, operand)][:],
-                        start=(k_pass == 0),
-                        stop=(k_pass == K_PASSES - 1),
-                    )
-                banks.append(z)
+                operand = operands[k_pass]
+                nc.tensor.matmul_mx(
+                    out=banks[f][:],
+                    lhsT=w_words[name][:, k_pass, cols].bitcast(FP8X4),
+                    lhsT_scale=w_planes[4 * k_pass : P, number, cols],
+                    rhs=x_codes[(j, operand)][:].bitcast(FP8X4),
+                    rhs_scale=x_planes[(j, operand)][:],
+                    start=(k_pass == 0),
+                    stop=(k_pass == K_PASSES - 1),
+                )
             return banks
 
         def activate(name, banks, bufs=1):
@@ -207,9 +264,12 @@ def tile_customlstmcell_kernel(
         def gate(j, name, bufs=1):
             return activate(name, multiply(j, name), bufs)
 
-        def combine(target, other, op):
-            for f in range(F_TILES):
-                nc.vector.tensor_tensor(out=target[:, f, :], in0=target[:, f, :], in1=other[:, f, :], op=op)
+        def combine(target, other, op, kind):
+            step = OPT["wide"][kind]
+            for f in range(0, F_TILES, step):
+                nc.vector.tensor_tensor(
+                    out=target[:, f : f + step, :], in0=target[:, f : f + step, :], in1=other[:, f : f + step, :], op=op
+                )
 
         def turn_back(source, block):
             bank = t_banks.tile([P, H], F32, tag="t")
@@ -219,6 +279,20 @@ def tile_customlstmcell_kernel(
                     in_=source[:, f, block * P : (block + 1) * P],
                     identity=identity[:],
                 )
+            return bank
+
+        def turn_back_sum(sources, block):
+            bank = t_banks.tile([P, H], F32, tag="t", name="bank")
+            for f in range(F_TILES):
+                for number, source in enumerate(sources):
+                    nc.tensor.matmul(
+                        out=bank[:, f * P : (f + 1) * P],
+                        lhsT=source[:, f, block * P : (block + 1) * P],
+                        rhs=identity[:],
+                        is_transpose=True,
+                        start=(number == 0),
+                        stop=(number == len(sources) - 1),
+                    )
             return bank
 
         def out_rows(dram, j, block):
@@ -247,7 +321,10 @@ def tile_customlstmcell_kernel(
                 tanh_tiles[block] = tanh_c
 
         def hidden_state(j, open_gate, tanh_tiles):
-            banks = [turn_back(open_gate, block) for block in range(BLOCKS)]
+            if isinstance(open_gate, tuple):
+                banks = [turn_back_sum(open_gate, block) for block in range(BLOCKS)]
+            else:
+                banks = [turn_back(open_gate, block) for block in range(BLOCKS)]
             for block in range(BLOCKS):
                 h_tile = rowwise.tile([P, H], F32, tag="h_new")
                 nc.vector.tensor_tensor(out=h_tile[:], in0=banks[block][:], in1=tanh_tiles[block][:], op=MULT)
@@ -257,42 +334,59 @@ def tile_customlstmcell_kernel(
             tanh_of_cell(LATE, c_tiles, tanh_tiles)
             hidden_state(j, open_gate, tanh_tiles)
 
-        transpose_x(0, "h_light")
-        transpose_x(0, "y")
+        transpose_x(0, "h_light", (nc.vector, nc.scalar))
         quantise_x(0, "h_light")
+        transpose_x(0, "y", (nc.scalar, nc.scalar))
+        transpose_biases(0)
         quantise_x(0, "y")
 
+        def prepare(behind):
+            items = OPT["prep"].get(behind, ())
+            for item in items:
+                if item == "bias":
+                    transpose_biases(1)
+                else:
+                    transpose_x(1, item)
+            for item in items:
+                if item != "bias":
+                    quantise_x(1, item)
+
         for j in range(N_CHUNKS):
-            banks = multiply(j, "i1")
-            if j == 0:
-                transpose_biases()
+            banks = multiply(j, "i1", pass_major=(j == 0 and OPT["pass_major_first"]))
             feed = activate("i1", banks, bufs=2)
             if j == 0:
                 transpose_x(0, "h_temp")
                 quantise_x(0, "h_temp")
-            combine(feed, gate(j, "c1"), MULT)
+                for operand in ("h_light", "y", "h_temp"):
+                    sort_x(1, operand)
+            combine(feed, gate(j, "c1"), MULT, "mult")
             if j == 0:
-                transpose_x(1, "h_light")
-                transpose_x(1, "y")
-                quantise_x(1, "h_light")
-                quantise_x(1, "y")
+                prepare("c1")
             else:
                 finish_chunk(*unfinished)
 
             feed_2 = gate(j, "i2")
             if j == 0:
-                transpose_x(1, "h_temp")
-                quantise_x(1, "h_temp")
-            combine(feed_2, gate(j, "c2"), MULT)
-            combine(feed, feed_2, ADD)
+                prepare("i2")
+            combine(feed_2, gate(j, "c2"), MULT, "mult")
+            if j == 0:
+                prepare("c2")
+            combine(feed, feed_2, ADD, "feed")
 
             keep = gate(j, "f1", bufs=2)
-            combine(keep, gate(j, "f2"), ADD)
+            if j == 0:
+                prepare("f1")
+            combine(keep, gate(j, "f2"), ADD, "keep")
+            if j == 0:
+                prepare("f2")
 
             open_gate = gate(j, "o1", bufs=2)
             c_tiles, tanh_tiles = {}, {}
             cell_state(j, keep, feed, EARLY, c_tiles)
-            combine(open_gate, gate(j, "o2"), ADD)
+            if j in OPT["open_on_pe"]:
+                open_gate = (open_gate, gate(j, "o2"))
+            else:
+                combine(open_gate, gate(j, "o2"), ADD, "open")
             tanh_of_cell(EARLY, c_tiles, tanh_tiles)
             cell_state(j, keep, feed, LATE, c_tiles)
             unfinished = (j, open_gate, c_tiles, tanh_tiles)

@@ -27,15 +27,16 @@ BANK = 512
 BANK_ROWS = BANK // 2
 
 OPT = {
-    "x0_pieces": 2,
-    "split_w_i1": True,
     "pass_major_first": True,
-    "early_biases": 4,
-    "loads": "h_temp0 c1 h_light1 i2 y1 c2 bias h_temp1 f1 f2 o1 c_light0 o2 c_light1",
-    "prep": {"c1": ("h_light",), "i2": ("y",), "c2": ("h_temp", "bias")},
+    "bias_bounds": (0, 4, 8), "bias0_on_scalar": False, "bias0_mid": True,
+    "loads": "h_light0.0 h_light0.1 sc.i1 y0.0 y0.1 w.i1.0 bias0 w.i1.1 h_temp0 c1 h_light1 i2 y1 c2 bias1 h_temp1 f1 f2 o1 c_light0 o2 c_light1",
+    "prep": {"c1": ("h_light",), "i2": ("y",), "c2": ("h_temp", "bias1")},
     "sorted": {},
-    "dummies": 0,
-    "open_on_pe": (),
+    "dummies": (0, 0, 0),
+    "pairs": False, "pair_stores": False,
+    "defer_q": False, "open_on_pool": (),
+    "tail_z": False, "tail_f_major": False, "tail_split": 1,
+    "open_on_pe": (1,),
     "wide": {"mult": 1, "feed": 1, "keep": 1, "open": 1},
 }
 
@@ -80,9 +81,12 @@ def tile_customlstmcell_kernel(
         t_banks = ctx.enter_context(tc.psum_pool(name="t_banks", bufs=4))
         ctx.enter_context(tc.manual_schedule())
 
-        bias_groups = (range(0, OPT["early_biases"]), range(OPT["early_biases"], len(gates)))
-        bias_rows = [resident.tile([P, P], BF16, name="bias_rows_%d" % group) for group in range(2)]
-        for group in range(2):
+        w_planes = resident.tile([P, len(gates), H], U8, name="w_planes", align_bytes=64)
+        nc.vector.memset(w_planes[:, 0, :].bitcast(I32), 0)
+        bounds = OPT["bias_bounds"]
+        bias_groups = [range(bounds[group], bounds[group + 1]) for group in range(len(bounds) - 1)]
+        bias_rows = [resident.tile([P, P], BF16, name="bias_rows_%d" % group) for group in range(len(bias_groups))]
+        for group in range(len(bias_groups)):
             nc.vector.memset(bias_rows[group][:], 0.0)
 
         def load_biases(group, queue):
@@ -92,14 +96,22 @@ def tile_customlstmcell_kernel(
                     in_=gates[number][3].rearrange("(f c) -> f c", c=P),
                 )
 
-        load_biases(0, nc.scalar)
+        if OPT["bias0_on_scalar"]:
+            load_biases(0, nc.scalar)
 
-        if OPT["dummies"]:
-            zeros = resident.tile([P, CHUNK], BF16, name="zeros")
-            nc.vector.memset(zeros[:], 0.0)
-            idle_bank = z_banks.tile([P, CHUNK], F32, tag="z", name="idle_bank")
-            for number in range(OPT["dummies"]):
-                nc.tensor.matmul(out=idle_bank[:], lhsT=zeros[:, 0:P], rhs=zeros[:], start=True, stop=True)
+        zeros = resident.tile([P, CHUNK], BF16, name="zeros")
+        idle_banks = []
+
+        def keep_warm(count, width=CHUNK):
+            if count and not idle_banks:
+                nc.vector.memset(zeros[:], 0.0)
+                idle_banks.append(z_banks.tile([P, CHUNK], F32, tag="z", name="idle_bank"))
+            for number in range(count):
+                nc.tensor.matmul(
+                    out=idle_banks[0][:, 0:width], lhsT=zeros[:, 0:P], rhs=zeros[:, 0:width], start=True, stop=True
+                )
+
+        keep_warm(OPT["dummies"][0])
 
         warm = resident.tile([P, 1], F32, name="warm")
         nc.vector.memset(warm[:], 0.0)
@@ -108,27 +120,31 @@ def tile_customlstmcell_kernel(
         identity = resident.tile([P, P], F32, name="identity")
         make_identity(nc, identity[:])
 
-        w_planes = resident.tile([P, len(gates), H], U8, name="w_planes", align_bytes=64)
-        nc.vector.memset(w_planes[:].bitcast(I32), 0)
+        nc.vector.memset(w_planes[:, 1:, :].bitcast(I32), 0)
 
-        x_raw, c_rows, w_words = {}, {}, {}
+        x_raw, c_rows, c_store, w_words = {}, {}, {}, {}
 
-        def load_rows(dram, j, name, pieces=1):
-            rows = resident.tile([P, BLOCKS, H], BF16, name="%s_%d" % (name, j))
+        def load_rows(store, dram, j, name, pieces=1, which=None):
+            if (j, name) not in store:
+                store[(j, name)] = resident.tile([P, BLOCKS, H], BF16, name="%s_%d" % (name, j))
+            rows = store[(j, name)]
             per = BLOCKS // pieces
-            for piece in range(pieces):
+            for piece in range(pieces) if which is None else (which,):
                 first = j * CHUNK + piece * per * P
-                nc.sync.dma_start(
-                    out=rows[:, piece * per : (piece + 1) * per, :],
-                    in_=dram[first : first + per * P, :].rearrange("(b p) k -> p b k", p=P),
-                )
-            return rows
-
-        def load_x(j, operand, pieces=1):
-            x_raw[(j, operand)] = load_rows(x_dram[operand], j, operand, pieces)
+                if OPT["pairs"]:
+                    nc.sync.dma_start(
+                        out=rows[:, piece * per : (piece + 1) * per, :].rearrange("p (h e) k -> p h e k", e=2),
+                        in_=dram[first : first + per * P, :].rearrange("(h p e) k -> p h e k", p=P, e=2),
+                    )
+                else:
+                    nc.sync.dma_start(
+                        out=rows[:, piece * per : (piece + 1) * per, :],
+                        in_=dram[first : first + per * P, :].rearrange("(b p) k -> p b k", p=P),
+                    )
 
         def load_c(j):
-            c_rows[j] = load_rows(c_light, j, "c_light")
+            load_rows(c_store, c_light, j, "c_light")
+            c_rows[j] = c_store[(j, "c_light")]
 
         def load_scales(name):
             number = gate_number[name]
@@ -160,27 +176,26 @@ def tile_customlstmcell_kernel(
             load_scales(name)
             load_words(name)
 
-        load_x(0, "h_light", OPT["x0_pieces"])
-        load_x(0, "y", OPT["x0_pieces"])
-        load_scales("i1")
-        if OPT["split_w_i1"]:
-            load_words("i1", 0)
-            load_words("i1", 1)
-        else:
-            load_words("i1")
         for token in OPT["loads"].split():
+            parts = token.split(".")
             if token in gate_number:
                 load_weight(token)
-            elif token == "bias":
-                load_biases(1, nc.sync)
+            elif parts[0] == "sc":
+                load_scales(parts[1])
+            elif parts[0] == "w":
+                load_words(parts[1], int(parts[2]))
+            elif token.startswith("bias"):
+                load_biases(int(token[-1]), nc.sync)
             elif token.startswith("c_light"):
                 load_c(int(token[-1]))
+            elif len(parts) == 2:
+                load_rows(x_raw, x_dram[parts[0][:-1]], int(parts[0][-1]), parts[0][:-1], 2, int(parts[1]))
             else:
-                load_x(int(token[-1]), token[:-1])
+                load_rows(x_raw, x_dram[token[:-1]], int(token[-1]), token[:-1])
 
         x_grouped, x_codes, x_planes, x_sorted = {}, {}, {}, {}
 
-        def transpose_x(j, operand, engines=(nc.vector, nc.scalar)):
+        def transpose_x(j, operand, engines=(nc.vector, nc.scalar), warm=0):
             grouped = stage.tile([P, 4 * CHUNK], BF16, tag="grouped", align_bytes=64)
             grouped_words = grouped[:].bitcast(F32).rearrange("p (r u) -> p r u", u=2)
             for bank in range(CHUNK // BANK_ROWS):
@@ -194,6 +209,7 @@ def tile_customlstmcell_kernel(
                             in_=x_sorted[(j, operand)][:, block, u, :] if (j, operand) in x_sorted else words[:, u : H // 2 : 2],
                             identity=identity[:],
                         )
+                keep_warm(warm, CHUNK // 2)
                 copy_out = engines[bank].tensor_copy if engines[bank] is nc.vector else engines[bank].copy
                 copy_out(
                     out=grouped_words[:, bank * BANK_ROWS : (bank + 1) * BANK_ROWS, :],
@@ -228,7 +244,7 @@ def tile_customlstmcell_kernel(
             cols = slice(F_TILES * bias_groups[group].start, F_TILES * bias_groups[group].stop)
             nc.scalar.copy(out=bias_cols[:, cols], in_=turned[:, cols])
 
-        def multiply(j, name, pass_major=False):
+        def multiply(j, name, pass_major=False, between=None):
             number = gate_number[name]
             banks = [z_banks.tile([P, CHUNK], F32, tag="z", name="z") for f in range(F_TILES)]
             operands = (gates[number][4], "y")
@@ -237,6 +253,8 @@ def tile_customlstmcell_kernel(
             else:
                 order = [(f, k_pass) for f in range(F_TILES) for k_pass in range(K_PASSES)]
             for f, k_pass in order:
+                if between is not None and (f, k_pass) == (0, 1):
+                    between()
                 cols = slice(f * P, (f + 1) * P)
                 operand = operands[k_pass]
                 nc.tensor.matmul_mx(
@@ -264,10 +282,10 @@ def tile_customlstmcell_kernel(
         def gate(j, name, bufs=1):
             return activate(name, multiply(j, name), bufs)
 
-        def combine(target, other, op, kind):
+        def combine(target, other, op, kind, engine=nc.vector):
             step = OPT["wide"][kind]
             for f in range(0, F_TILES, step):
-                nc.vector.tensor_tensor(
+                engine.tensor_tensor(
                     out=target[:, f : f + step, :], in0=target[:, f : f + step, :], in1=other[:, f : f + step, :], op=op
                 )
 
@@ -281,23 +299,16 @@ def tile_customlstmcell_kernel(
                 )
             return bank
 
-        def turn_back_sum(sources, block):
-            bank = t_banks.tile([P, H], F32, tag="t", name="bank")
-            for f in range(F_TILES):
-                for number, source in enumerate(sources):
-                    nc.tensor.matmul(
-                        out=bank[:, f * P : (f + 1) * P],
-                        lhsT=source[:, f, block * P : (block + 1) * P],
-                        rhs=identity[:],
-                        is_transpose=True,
-                        start=(number == 0),
-                        stop=(number == len(sources) - 1),
-                    )
-            return bank
-
         def out_rows(dram, j, block):
+            if OPT["pairs"]:
+                first = j * CHUNK + (block // 2) * 2 * P
+                return dram[first : first + 2 * P, :].rearrange("(p e) k -> p e k", e=2)[:, block % 2, :]
             first = j * CHUNK + block * P
             return dram[first : first + P, :]
+
+        def out_pair(dram, j, half):
+            first = j * CHUNK + half * 2 * P
+            return dram[first : first + 2 * P, :].rearrange("(p e) k -> p e k", e=2)
 
         def cell_state(j, keep, feed, blocks, c_tiles):
             keep_banks = {block: turn_back(keep, block) for block in blocks}
@@ -308,70 +319,121 @@ def tile_customlstmcell_kernel(
                 nc.vector.tensor_tensor(
                     out=kept[block][:], in0=keep_banks[block][:], in1=c_rows[j][:, block, :], op=MULT
                 )
+            c_pair = rowwise.tile([P, 2, H], F32, tag="c_new", name="c_pair", bufs=2)
+            together = OPT["pair_stores"] and not (j == N_CHUNKS - 1 and blocks == LATE)
             for block in blocks:
-                c_tile = rowwise.tile([P, H], F32, tag="c_new")
-                nc.vector.tensor_tensor(out=c_tile[:], in0=feed_banks[block][:], in1=kept[block][:], op=ADD)
-                nc.sync.dma_start(out=out_rows(c_new, j, block), in_=c_tile[:])
+                c_tile = c_pair[:, block % 2, :]
+                nc.vector.tensor_tensor(out=c_tile, in0=feed_banks[block][:], in1=kept[block][:], op=ADD)
+                if not together:
+                    nc.sync.dma_start(out=out_rows(c_new, j, block), in_=c_tile)
                 c_tiles[block] = c_tile
+            if together:
+                nc.sync.dma_start(out=out_pair(c_new, j, blocks[0] // 2), in_=c_pair[:])
 
         def tanh_of_cell(blocks, c_tiles, tanh_tiles):
             for block in blocks:
                 tanh_c = rowwise.tile([P, H], F32, tag="tanh_c")
-                nc.scalar.activation(out=tanh_c[:], in_=c_tiles[block][:], func=TANH)
+                nc.scalar.activation(out=tanh_c[:], in_=c_tiles[block], func=TANH)
                 tanh_tiles[block] = tanh_c
 
         def hidden_state(j, open_gate, tanh_tiles):
-            if isinstance(open_gate, tuple):
-                banks = [turn_back_sum(open_gate, block) for block in range(BLOCKS)]
+            last = j == N_CHUNKS - 1
+            sources = open_gate if isinstance(open_gate, tuple) else (open_gate,)
+            if last and OPT["tail_z"]:
+                banks = [z_banks.tile([P, H], F32, tag="z", name="open_bank") for block in range(BLOCKS)]
             else:
-                banks = [turn_back(open_gate, block) for block in range(BLOCKS)]
+                banks = [t_banks.tile([P, H], F32, tag="t", name="open_bank") for block in range(BLOCKS)]
+            if last and OPT["tail_f_major"]:
+                order = [(block, f) for f in range(F_TILES) for block in range(BLOCKS)]
+            else:
+                order = [(block, f) for block in range(BLOCKS) for f in range(F_TILES)]
+            for block, f in order:
+                for number, source in enumerate(sources):
+                    nc.tensor.matmul(
+                        out=banks[block][:, f * P : (f + 1) * P],
+                        lhsT=source[:, f, block * P : (block + 1) * P],
+                        rhs=identity[:],
+                        is_transpose=True,
+                        start=(number == 0),
+                        stop=(number == len(sources) - 1),
+                    )
             for block in range(BLOCKS):
-                h_tile = rowwise.tile([P, H], F32, tag="h_new")
-                nc.vector.tensor_tensor(out=h_tile[:], in0=banks[block][:], in1=tanh_tiles[block][:], op=MULT)
-                nc.sync.dma_start(out=out_rows(h_new, j, block), in_=h_tile[:])
+                if block % 2 == 0:
+                    h_pair = rowwise.tile([P, 2, H], F32, tag="h_new", name="h_pair", bufs=2)
+                h_tile = h_pair[:, block % 2, :]
+                together = OPT["pair_stores"] and not last
+                pieces = OPT["tail_split"] if last and block == BLOCKS - 1 else 1
+                for piece in range(pieces):
+                    cols = slice(piece * H // pieces, (piece + 1) * H // pieces)
+                    nc.vector.tensor_tensor(
+                        out=h_tile[:, cols], in0=banks[block][:, cols], in1=tanh_tiles[block][:, cols], op=MULT
+                    )
+                    if not together:
+                        nc.sync.dma_start(out=out_rows(h_new, j, block)[:, cols], in_=h_tile[:, cols])
+                if together and block % 2 == 1:
+                    nc.sync.dma_start(out=out_pair(h_new, j, block // 2), in_=h_pair[:])
 
         def finish_chunk(j, open_gate, c_tiles, tanh_tiles):
             tanh_of_cell(LATE, c_tiles, tanh_tiles)
             hidden_state(j, open_gate, tanh_tiles)
 
-        transpose_x(0, "h_light", (nc.vector, nc.scalar))
+        transpose_x(0, "h_light", (nc.vector, nc.scalar), OPT["dummies"][1])
         quantise_x(0, "h_light")
-        transpose_x(0, "y", (nc.scalar, nc.scalar))
-        transpose_biases(0)
+        transpose_x(0, "y", (nc.scalar, nc.scalar), OPT["dummies"][1])
+        if not OPT["bias0_mid"]:
+            transpose_biases(0)
+        keep_warm(OPT["dummies"][2])
         quantise_x(0, "y")
+        sort_x(0, "h_temp")
+
+        waiting = []
 
         def prepare(behind):
             items = OPT["prep"].get(behind, ())
             for item in items:
-                if item == "bias":
-                    transpose_biases(1)
+                if item.startswith("bias"):
+                    transpose_biases(int(item[-1]))
                 else:
                     transpose_x(1, item)
-            for item in items:
-                if item != "bias":
+            if OPT["defer_q"]:
+                for item in waiting:
                     quantise_x(1, item)
+                waiting.clear()
+            for item in items:
+                if not item.startswith("bias"):
+                    if OPT["defer_q"]:
+                        waiting.append(item)
+                    else:
+                        quantise_x(1, item)
 
         for j in range(N_CHUNKS):
-            banks = multiply(j, "i1", pass_major=(j == 0 and OPT["pass_major_first"]))
+            banks = multiply(
+                j, "i1", pass_major=(j == 0 and OPT["pass_major_first"]),
+                between=(lambda: transpose_biases(0)) if j == 0 and OPT["bias0_mid"] else None,
+            )
             feed = activate("i1", banks, bufs=2)
             if j == 0:
                 transpose_x(0, "h_temp")
+                prepare("i1")
                 quantise_x(0, "h_temp")
-                for operand in ("h_light", "y", "h_temp"):
-                    sort_x(1, operand)
+                sort_x(1, "h_light")
             combine(feed, gate(j, "c1"), MULT, "mult")
             if j == 0:
                 prepare("c1")
+                sort_x(1, "y")
             else:
                 finish_chunk(*unfinished)
 
             feed_2 = gate(j, "i2")
             if j == 0:
                 prepare("i2")
+                sort_x(1, "h_temp")
             combine(feed_2, gate(j, "c2"), MULT, "mult")
             if j == 0:
                 prepare("c2")
             combine(feed, feed_2, ADD, "feed")
+            if j == 0:
+                prepare("feed")
 
             keep = gate(j, "f1", bufs=2)
             if j == 0:
@@ -386,7 +448,7 @@ def tile_customlstmcell_kernel(
             if j in OPT["open_on_pe"]:
                 open_gate = (open_gate, gate(j, "o2"))
             else:
-                combine(open_gate, gate(j, "o2"), ADD, "open")
+                combine(open_gate, gate(j, "o2"), ADD, "open", nc.gpsimd if j in OPT["open_on_pool"] else nc.vector)
             tanh_of_cell(EARLY, c_tiles, tanh_tiles)
             cell_state(j, keep, feed, LATE, c_tiles)
             unfinished = (j, open_gate, c_tiles, tanh_tiles)

@@ -35,7 +35,10 @@ OPT = {
     "dummies": (0, 0, 0),
     "pairs": False, "pair_stores": False,
     "defer_q": False, "open_on_pool": (),
-    "tail_z": False, "tail_f_major": False, "tail_split": 1,
+    "tail_z": False, "tail_f_major": False, "tail_split": 1, "tail_two_banks": False,
+    "keep_ahead": True,
+    "head_halves": False, "head_copies": ("VS", "SS"),
+    "open_pe_tiles": (0, 1, 2, 3),
     "open_on_pe": (1,),
     "wide": {"mult": 1, "feed": 1, "keep": 1, "open": 1},
 }
@@ -156,12 +159,18 @@ def tile_customlstmcell_kernel(
                     in_=scales_dram[:, 4 * quadrant : 4 * quadrant + 4, :].bitcast(I32),
                 )
 
-        def load_words(name, k_pass=None):
+        def load_words(name, k_pass=None, half=None):
             words_dram = gates[gate_number[name]][1]
             if name not in w_words:
                 w_words[name] = resident.tile([P, K_PASSES, H], U32, name="words_%s" % name, align_bytes=64)
             words = w_words[name]
-            if k_pass is None:
+            if half is not None:
+                cols = slice(half * H // 2, (half + 1) * H // 2)
+                nc.sync.dma_start(
+                    out=words[:, k_pass, cols].bitcast(I32),
+                    in_=words_dram[k_pass, :, cols, :].rearrange("p n t -> p (n t)").bitcast(I32),
+                )
+            elif k_pass is None:
                 nc.sync.dma_start(
                     out=words[:].bitcast(I32),
                     in_=words_dram.rearrange("g p n t -> p g (n t)").bitcast(I32),
@@ -182,6 +191,8 @@ def tile_customlstmcell_kernel(
                 load_weight(token)
             elif parts[0] == "sc":
                 load_scales(parts[1])
+            elif parts[0] == "w" and len(parts) == 4:
+                load_words(parts[1], int(parts[2]), int(parts[3]))
             elif parts[0] == "w":
                 load_words(parts[1], int(parts[2]))
             elif token.startswith("bias"):
@@ -194,8 +205,9 @@ def tile_customlstmcell_kernel(
                 load_rows(x_raw, x_dram[token[:-1]], int(token[-1]), token[:-1])
 
         x_grouped, x_codes, x_planes, x_sorted = {}, {}, {}, {}
+        OPT_ENGINES = {"VS": (nc.vector, nc.scalar), "SS": (nc.scalar, nc.scalar), "SV": (nc.scalar, nc.vector), "VV": (nc.vector, nc.vector)}
 
-        def transpose_x(j, operand, engines=(nc.vector, nc.scalar), warm=0):
+        def transpose_x(j, operand, engines=(nc.vector, nc.scalar), warm=0, halves=False):
             grouped = stage.tile([P, 4 * CHUNK], BF16, tag="grouped", align_bytes=64)
             grouped_words = grouped[:].bitcast(F32).rearrange("p (r u) -> p r u", u=2)
             for bank in range(CHUNK // BANK_ROWS):
@@ -215,6 +227,9 @@ def tile_customlstmcell_kernel(
                     out=grouped_words[:, bank * BANK_ROWS : (bank + 1) * BANK_ROWS, :],
                     in_=turned[:].rearrange("p u r -> p r u"),
                 )
+                if halves:
+                    x_grouped[(j, operand)] = grouped
+                    quantise_x(j, operand, bank)
             x_grouped[(j, operand)] = grouped
 
         def sort_x(j, operand):
@@ -226,13 +241,16 @@ def tile_customlstmcell_kernel(
                 )
                 x_sorted[(j, operand)] = ordered
 
-        def quantise_x(j, operand):
-            codes = resident.tile([P, CHUNK], U32, name="codes_%s_%d" % (operand, j), align_bytes=64)
-            plane = resident.tile([P, CHUNK], U8, name="plane_%s_%d" % (operand, j), align_bytes=64)
+        def quantise_x(j, operand, part=None):
+            if (j, operand) not in x_codes:
+                x_codes[(j, operand)] = resident.tile([P, CHUNK], U32, name="codes_%s_%d" % (operand, j), align_bytes=64)
+                x_planes[(j, operand)] = resident.tile([P, CHUNK], U8, name="plane_%s_%d" % (operand, j), align_bytes=64)
+            codes, plane = x_codes[(j, operand)], x_planes[(j, operand)]
+            rows = slice(0, CHUNK) if part is None else slice(part * BANK_ROWS, (part + 1) * BANK_ROWS)
             nc.vector.quantize_mx(
-                out=codes[:].bitcast(FP8X4), scales=plane[:], in_=x_grouped[(j, operand)][:]
+                out=codes[:, rows].bitcast(FP8X4), scales=plane[:, rows],
+                in_=x_grouped[(j, operand)][:, 4 * rows.start : 4 * rows.stop],
             )
-            x_codes[(j, operand)], x_planes[(j, operand)] = codes, plane
 
         bias_cols = resident.tile([P, P], F32, name="bias_cols")
 
@@ -289,8 +307,11 @@ def tile_customlstmcell_kernel(
                     out=target[:, f : f + step, :], in0=target[:, f : f + step, :], in1=other[:, f : f + step, :], op=op
                 )
 
-        def turn_back(source, block):
-            bank = t_banks.tile([P, H], F32, tag="t")
+        def turn_back(source, block, spare=False):
+            if spare:
+                bank = z_banks.tile([P, H], F32, tag="z", name="spare_bank")
+            else:
+                bank = t_banks.tile([P, H], F32, tag="t", name="bank")
             for f in range(F_TILES):
                 nc.tensor.transpose(
                     out=bank[:, f * P : (f + 1) * P],
@@ -310,12 +331,17 @@ def tile_customlstmcell_kernel(
             first = j * CHUNK + half * 2 * P
             return dram[first : first + 2 * P, :].rearrange("(p e) k -> p e k", e=2)
 
+        kept = {}
+
         def cell_state(j, keep, feed, blocks, c_tiles):
-            keep_banks = {block: turn_back(keep, block) for block in blocks}
+            ahead = OPT["keep_ahead"] and j == N_CHUNKS - 1
+            keep_banks = {} if ahead and blocks == LATE else {block: turn_back(keep, block) for block in blocks}
             feed_banks = {block: turn_back(feed, block) for block in blocks}
-            kept = {}
-            for block in blocks:
-                kept[block] = rowwise.tile([P, H], F32, tag="kept", name="kept", bufs=2)
+            if ahead and blocks == EARLY:
+                for block in LATE:
+                    keep_banks[block] = turn_back(keep, block, spare=True)
+            for block in sorted(keep_banks):
+                kept[block] = rowwise.tile([P, H], F32, tag="kept", name="kept", bufs=4 if OPT["keep_ahead"] else 2)
                 nc.vector.tensor_tensor(
                     out=kept[block][:], in0=keep_banks[block][:], in1=c_rows[j][:, block, :], op=MULT
                 )
@@ -347,15 +373,20 @@ def tile_customlstmcell_kernel(
                 order = [(block, f) for f in range(F_TILES) for block in range(BLOCKS)]
             else:
                 order = [(block, f) for block in range(BLOCKS) for f in range(F_TILES)]
+            two_banks = last and OPT["tail_two_banks"]
+            if two_banks:
+                extra = z_banks.tile([P, H], F32, tag="z", name="extra_bank")
             for block, f in order:
-                for number, source in enumerate(sources):
+                summed = sources if f in OPT["open_pe_tiles"] else sources[:1]
+                in_extra = two_banks and block == BLOCKS - 1 and f >= F_TILES // 2
+                for number, source in enumerate(summed):
                     nc.tensor.matmul(
-                        out=banks[block][:, f * P : (f + 1) * P],
+                        out=extra[:, (f - F_TILES // 2) * P : (f - F_TILES // 2 + 1) * P] if in_extra else banks[block][:, f * P : (f + 1) * P],
                         lhsT=source[:, f, block * P : (block + 1) * P],
                         rhs=identity[:],
                         is_transpose=True,
                         start=(number == 0),
-                        stop=(number == len(sources) - 1),
+                        stop=(number == len(summed) - 1),
                     )
             for block in range(BLOCKS):
                 if block % 2 == 0:
@@ -366,7 +397,9 @@ def tile_customlstmcell_kernel(
                 for piece in range(pieces):
                     cols = slice(piece * H // pieces, (piece + 1) * H // pieces)
                     nc.vector.tensor_tensor(
-                        out=h_tile[:, cols], in0=banks[block][:, cols], in1=tanh_tiles[block][:, cols], op=MULT
+                        out=h_tile[:, cols],
+                        in0=extra[:, 0 : H // 2] if two_banks and pieces == 2 and piece == 1 else banks[block][:, cols],
+                        in1=tanh_tiles[block][:, cols], op=MULT,
                     )
                     if not together:
                         nc.sync.dma_start(out=out_rows(h_new, j, block)[:, cols], in_=h_tile[:, cols])
@@ -377,13 +410,15 @@ def tile_customlstmcell_kernel(
             tanh_of_cell(LATE, c_tiles, tanh_tiles)
             hidden_state(j, open_gate, tanh_tiles)
 
-        transpose_x(0, "h_light", (nc.vector, nc.scalar), OPT["dummies"][1])
-        quantise_x(0, "h_light")
-        transpose_x(0, "y", (nc.scalar, nc.scalar), OPT["dummies"][1])
+        transpose_x(0, "h_light", OPT_ENGINES[OPT["head_copies"][0]], OPT["dummies"][1], OPT["head_halves"])
+        if not OPT["head_halves"]:
+            quantise_x(0, "h_light")
+        transpose_x(0, "y", OPT_ENGINES[OPT["head_copies"][1]], OPT["dummies"][1], OPT["head_halves"])
         if not OPT["bias0_mid"]:
             transpose_biases(0)
         keep_warm(OPT["dummies"][2])
-        quantise_x(0, "y")
+        if not OPT["head_halves"]:
+            quantise_x(0, "y")
         sort_x(0, "h_temp")
 
         waiting = []
@@ -446,7 +481,13 @@ def tile_customlstmcell_kernel(
             c_tiles, tanh_tiles = {}, {}
             cell_state(j, keep, feed, EARLY, c_tiles)
             if j in OPT["open_on_pe"]:
-                open_gate = (open_gate, gate(j, "o2"))
+                second = gate(j, "o2")
+                for f in range(F_TILES):
+                    if f not in OPT["open_pe_tiles"]:
+                        nc.vector.tensor_tensor(
+                            out=open_gate[:, f, :], in0=open_gate[:, f, :], in1=second[:, f, :], op=ADD
+                        )
+                open_gate = (open_gate, second)
             else:
                 combine(open_gate, gate(j, "o2"), ADD, "open", nc.gpsimd if j in OPT["open_on_pool"] else nc.vector)
             tanh_of_cell(EARLY, c_tiles, tanh_tiles)

@@ -21,27 +21,12 @@ K_PASSES = 2
 F_TILES = H // P
 CHUNK = 512
 N_CHUNKS = ROWS // CHUNK
+LAST = N_CHUNKS - 1
 BLOCKS = CHUNK // P
 EARLY, LATE = (0, 1), (2, 3)
 BANK = 512
 BANK_ROWS = BANK // 2
-
-OPT = {
-    "pass_major_first": True,
-    "bias_bounds": (0, 4, 8), "bias0_on_scalar": False, "bias0_mid": True,
-    "loads": "h_light0.0 h_light0.1 sc.i1 y0.0 y0.1 w.i1.0 bias0 w.i1.1 h_temp0 c1 h_light1 i2 y1 c2 bias1 h_temp1 f1 f2 o1 c_light0 o2 c_light1",
-    "prep": {"c1": ("h_light",), "i2": ("y",), "c2": ("h_temp", "bias1")},
-    "sorted": {},
-    "dummies": (0, 0, 0),
-    "pairs": False, "pair_stores": False,
-    "defer_q": False, "open_on_pool": (),
-    "tail_z": False, "tail_f_major": False, "tail_split": 1, "tail_two_banks": False,
-    "keep_ahead": True,
-    "head_halves": False, "head_copies": ("VS", "SS"),
-    "open_pe_tiles": (0, 1, 2, 3),
-    "open_on_pe": (1,),
-    "wide": {"mult": 1, "feed": 1, "keep": 1, "open": 1},
-}
+GATES_IN_BIAS_GROUP = 4
 
 FLOPS = 2 * ROWS * (2 * H) * (8 * H)
 BYTES = 4 * ROWS * H * 2 + 8 * (2 * H * H + 2 * 16 * H + H * 2) + 2 * ROWS * H * 4
@@ -74,6 +59,7 @@ def tile_customlstmcell_kernel(
         ("o2", w_o_light_temp_words, w_o_light_temp_scales, b_o_light_temp, "h_temp", SIGMOID),
     )
     gate_number = {gate[0]: number for number, gate in enumerate(gates)}
+    bias_groups = len(gates) // GATES_IN_BIAS_GROUP
 
     with ExitStack() as ctx:
         resident = ctx.enter_context(tc.tile_pool(name="resident", bufs=1))
@@ -86,35 +72,10 @@ def tile_customlstmcell_kernel(
 
         w_planes = resident.tile([P, len(gates), H], U8, name="w_planes", align_bytes=64)
         nc.vector.memset(w_planes[:, 0, :].bitcast(I32), 0)
-        bounds = OPT["bias_bounds"]
-        bias_groups = [range(bounds[group], bounds[group + 1]) for group in range(len(bounds) - 1)]
-        bias_rows = [resident.tile([P, P], BF16, name="bias_rows_%d" % group) for group in range(len(bias_groups))]
-        for group in range(len(bias_groups)):
+
+        bias_rows = [resident.tile([P, P], BF16, name="bias_rows_%d" % group) for group in range(bias_groups)]
+        for group in range(bias_groups):
             nc.vector.memset(bias_rows[group][:], 0.0)
-
-        def load_biases(group, queue):
-            for number in bias_groups[group]:
-                queue.dma_start(
-                    out=bias_rows[group][F_TILES * number : F_TILES * (number + 1), :],
-                    in_=gates[number][3].rearrange("(f c) -> f c", c=P),
-                )
-
-        if OPT["bias0_on_scalar"]:
-            load_biases(0, nc.scalar)
-
-        zeros = resident.tile([P, CHUNK], BF16, name="zeros")
-        idle_banks = []
-
-        def keep_warm(count, width=CHUNK):
-            if count and not idle_banks:
-                nc.vector.memset(zeros[:], 0.0)
-                idle_banks.append(z_banks.tile([P, CHUNK], F32, tag="z", name="idle_bank"))
-            for number in range(count):
-                nc.tensor.matmul(
-                    out=idle_banks[0][:, 0:width], lhsT=zeros[:, 0:P], rhs=zeros[:, 0:width], start=True, stop=True
-                )
-
-        keep_warm(OPT["dummies"][0])
 
         warm = resident.tile([P, 1], F32, name="warm")
         nc.vector.memset(warm[:], 0.0)
@@ -125,165 +86,147 @@ def tile_customlstmcell_kernel(
 
         nc.vector.memset(w_planes[:, 1:, :].bitcast(I32), 0)
 
-        x_raw, c_rows, c_store, w_words = {}, {}, {}, {}
+        x_raw, c_rows, w_words = {}, {}, {}
 
-        def load_rows(store, dram, j, name, pieces=1, which=None):
-            if (j, name) not in store:
-                store[(j, name)] = resident.tile([P, BLOCKS, H], BF16, name="%s_%d" % (name, j))
-            rows = store[(j, name)]
-            per = BLOCKS // pieces
-            for piece in range(pieces) if which is None else (which,):
-                first = j * CHUNK + piece * per * P
-                if OPT["pairs"]:
-                    nc.sync.dma_start(
-                        out=rows[:, piece * per : (piece + 1) * per, :].rearrange("p (h e) k -> p h e k", e=2),
-                        in_=dram[first : first + per * P, :].rearrange("(h p e) k -> p h e k", p=P, e=2),
-                    )
-                else:
-                    nc.sync.dma_start(
-                        out=rows[:, piece * per : (piece + 1) * per, :],
-                        in_=dram[first : first + per * P, :].rearrange("(b p) k -> p b k", p=P),
-                    )
+        def load_rows(dram, j, name, pieces=1):
+            rows = resident.tile([P, BLOCKS, H], BF16, name="%s_%d" % (name, j))
+            blocks = BLOCKS // pieces
+            for piece in range(pieces):
+                first = j * CHUNK + piece * blocks * P
+                nc.sync.dma_start(
+                    out=rows[:, piece * blocks : (piece + 1) * blocks, :],
+                    in_=dram[first : first + blocks * P, :].rearrange("(b p) k -> p b k", p=P),
+                )
+            return rows
+
+        def load_x(j, operand, pieces=1):
+            x_raw[(j, operand)] = load_rows(x_dram[operand], j, operand, pieces)
 
         def load_c(j):
-            load_rows(c_store, c_light, j, "c_light")
-            c_rows[j] = c_store[(j, "c_light")]
+            c_rows[j] = load_rows(c_light, j, "c_light")
 
         def load_scales(name):
             number = gate_number[name]
-            scales_dram = gates[number][2]
             for quadrant in range(4):
                 first = 32 * quadrant
                 nc.sync.dma_start(
                     out=w_planes[first : first + 4 * K_PASSES, number, :].bitcast(I32),
-                    in_=scales_dram[:, 4 * quadrant : 4 * quadrant + 4, :].bitcast(I32),
+                    in_=gates[number][2][:, 4 * quadrant : 4 * quadrant + 4, :].bitcast(I32),
                 )
 
-        def load_words(name, k_pass=None, half=None):
-            words_dram = gates[gate_number[name]][1]
+        def load_words(name, k_passes):
             if name not in w_words:
                 w_words[name] = resident.tile([P, K_PASSES, H], U32, name="words_%s" % name, align_bytes=64)
-            words = w_words[name]
-            if half is not None:
-                cols = slice(half * H // 2, (half + 1) * H // 2)
-                nc.sync.dma_start(
-                    out=words[:, k_pass, cols].bitcast(I32),
-                    in_=words_dram[k_pass, :, cols, :].rearrange("p n t -> p (n t)").bitcast(I32),
-                )
-            elif k_pass is None:
-                nc.sync.dma_start(
-                    out=words[:].bitcast(I32),
-                    in_=words_dram.rearrange("g p n t -> p g (n t)").bitcast(I32),
-                )
-            else:
-                nc.sync.dma_start(
-                    out=words[:, k_pass, :].bitcast(I32),
-                    in_=words_dram[k_pass].rearrange("p n t -> p (n t)").bitcast(I32),
-                )
+            nc.sync.dma_start(
+                out=w_words[name][:, k_passes, :].bitcast(I32),
+                in_=gates[gate_number[name]][1][k_passes].rearrange("g p n t -> p g (n t)").bitcast(I32),
+            )
 
         def load_weight(name):
             load_scales(name)
-            load_words(name)
+            load_words(name, slice(0, K_PASSES))
 
-        for token in OPT["loads"].split():
-            parts = token.split(".")
-            if token in gate_number:
-                load_weight(token)
-            elif parts[0] == "sc":
-                load_scales(parts[1])
-            elif parts[0] == "w" and len(parts) == 4:
-                load_words(parts[1], int(parts[2]), int(parts[3]))
-            elif parts[0] == "w":
-                load_words(parts[1], int(parts[2]))
-            elif token.startswith("bias"):
-                load_biases(int(token[-1]), nc.sync)
-            elif token.startswith("c_light"):
-                load_c(int(token[-1]))
-            elif len(parts) == 2:
-                load_rows(x_raw, x_dram[parts[0][:-1]], int(parts[0][-1]), parts[0][:-1], 2, int(parts[1]))
-            else:
-                load_rows(x_raw, x_dram[token[:-1]], int(token[-1]), token[:-1])
+        def load_biases(group):
+            for number in range(group * GATES_IN_BIAS_GROUP, (group + 1) * GATES_IN_BIAS_GROUP):
+                nc.sync.dma_start(
+                    out=bias_rows[group][F_TILES * number : F_TILES * (number + 1), :],
+                    in_=gates[number][3].rearrange("(f c) -> f c", c=P),
+                )
 
-        x_grouped, x_codes, x_planes, x_sorted = {}, {}, {}, {}
-        OPT_ENGINES = {"VS": (nc.vector, nc.scalar), "SS": (nc.scalar, nc.scalar), "SV": (nc.scalar, nc.vector), "VV": (nc.vector, nc.vector)}
+        load_x(0, "h_light", pieces=2)
+        load_scales("i1")
+        load_x(0, "y", pieces=2)
+        load_words("i1", slice(0, 1))
+        load_biases(0)
+        load_words("i1", slice(1, 2))
+        load_x(0, "h_temp")
+        load_weight("c1")
+        load_x(1, "h_light")
+        load_weight("i2")
+        load_x(1, "y")
+        load_weight("c2")
+        load_biases(1)
+        load_x(1, "h_temp")
+        load_weight("f1")
+        load_weight("f2")
+        load_weight("o1")
+        load_c(0)
+        load_weight("o2")
+        load_c(1)
 
-        def transpose_x(j, operand, engines=(nc.vector, nc.scalar), warm=0, halves=False):
+        x_grouped, x_codes, x_planes = {}, {}, {}
+
+        def transpose_x(j, operand, copy_engines=(nc.vector, nc.scalar)):
             grouped = stage.tile([P, 4 * CHUNK], BF16, tag="grouped", align_bytes=64)
             grouped_words = grouped[:].bitcast(F32).rearrange("p (r u) -> p r u", u=2)
             for bank in range(CHUNK // BANK_ROWS):
                 turned = t_banks.tile([P, 2, BANK_ROWS], F32, tag="t")
                 for half in range(BANK_ROWS // P):
-                    block = bank * (BANK_ROWS // P) + half
-                    words = x_raw[(j, operand)][:, block, :].bitcast(F32)
+                    words = x_raw[(j, operand)][:, bank * (BANK_ROWS // P) + half, :].bitcast(F32)
                     for u in range(2):
                         nc.tensor.transpose(
                             out=turned[:, u, half * P : (half + 1) * P],
-                            in_=x_sorted[(j, operand)][:, block, u, :] if (j, operand) in x_sorted else words[:, u : H // 2 : 2],
+                            in_=words[:, u : H // 2 : 2],
                             identity=identity[:],
                         )
-                keep_warm(warm, CHUNK // 2)
-                copy_out = engines[bank].tensor_copy if engines[bank] is nc.vector else engines[bank].copy
+                engine = copy_engines[bank]
+                copy_out = engine.tensor_copy if engine is nc.vector else engine.copy
                 copy_out(
                     out=grouped_words[:, bank * BANK_ROWS : (bank + 1) * BANK_ROWS, :],
                     in_=turned[:].rearrange("p u r -> p r u"),
                 )
-                if halves:
-                    x_grouped[(j, operand)] = grouped
-                    quantise_x(j, operand, bank)
             x_grouped[(j, operand)] = grouped
 
-        def sort_x(j, operand):
-            if (j, operand) in OPT["sorted"]:
-                engine = {"gpsimd": nc.gpsimd, "vector": nc.vector}[OPT["sorted"][(j, operand)]]
-                ordered = stage.tile([P, BLOCKS, 2, P], F32, tag="ordered", name="ordered")
-                engine.tensor_copy(
-                    out=ordered[:], in_=x_raw[(j, operand)][:].bitcast(F32).rearrange("p b (w u) -> p b u w", u=2)
-                )
-                x_sorted[(j, operand)] = ordered
-
-        def quantise_x(j, operand, part=None):
-            if (j, operand) not in x_codes:
-                x_codes[(j, operand)] = resident.tile([P, CHUNK], U32, name="codes_%s_%d" % (operand, j), align_bytes=64)
-                x_planes[(j, operand)] = resident.tile([P, CHUNK], U8, name="plane_%s_%d" % (operand, j), align_bytes=64)
-            codes, plane = x_codes[(j, operand)], x_planes[(j, operand)]
-            rows = slice(0, CHUNK) if part is None else slice(part * BANK_ROWS, (part + 1) * BANK_ROWS)
+        def quantise_x(j, operand):
+            codes = resident.tile([P, CHUNK], U32, name="codes_%s_%d" % (operand, j), align_bytes=64)
+            plane = resident.tile([P, CHUNK], U8, name="plane_%s_%d" % (operand, j), align_bytes=64)
             nc.vector.quantize_mx(
-                out=codes[:, rows].bitcast(FP8X4), scales=plane[:, rows],
-                in_=x_grouped[(j, operand)][:, 4 * rows.start : 4 * rows.stop],
+                out=codes[:].bitcast(FP8X4), scales=plane[:], in_=x_grouped[(j, operand)][:]
             )
+            x_codes[(j, operand)], x_planes[(j, operand)] = codes, plane
+
+        def prepare_x(j, operand):
+            transpose_x(j, operand)
+            quantise_x(j, operand)
 
         bias_cols = resident.tile([P, P], F32, name="bias_cols")
 
         def transpose_biases(group):
             bias_f32 = resident.tile([P, P], F32, name="bias_f32_%d" % group)
             nc.gpsimd.tensor_copy(out=bias_f32[:], in_=bias_rows[group][:])
-            turned = t_banks.tile([P, P], F32, tag="t", name="turned_bias")
+            turned = t_banks.tile([P, P], F32, tag="t")
             nc.tensor.transpose(out=turned[:], in_=bias_f32[:], identity=identity[:])
-            cols = slice(F_TILES * bias_groups[group].start, F_TILES * bias_groups[group].stop)
+            width = F_TILES * GATES_IN_BIAS_GROUP
+            cols = slice(group * width, (group + 1) * width)
             nc.scalar.copy(out=bias_cols[:, cols], in_=turned[:, cols])
 
-        def multiply(j, name, pass_major=False, between=None):
+        def multiply(j, name, between_passes=None):
             number = gate_number[name]
-            banks = [z_banks.tile([P, CHUNK], F32, tag="z", name="z") for f in range(F_TILES)]
             operands = (gates[number][4], "y")
-            if pass_major:
-                order = [(f, k_pass) for k_pass in range(K_PASSES) for f in range(F_TILES)]
-            else:
-                order = [(f, k_pass) for f in range(F_TILES) for k_pass in range(K_PASSES)]
-            for f, k_pass in order:
-                if between is not None and (f, k_pass) == (0, 1):
-                    between()
+            banks = [z_banks.tile([P, CHUNK], F32, tag="z", name="z") for f in range(F_TILES)]
+
+            def one_pass(f, k_pass):
                 cols = slice(f * P, (f + 1) * P)
-                operand = operands[k_pass]
                 nc.tensor.matmul_mx(
                     out=banks[f][:],
                     lhsT=w_words[name][:, k_pass, cols].bitcast(FP8X4),
                     lhsT_scale=w_planes[4 * k_pass : P, number, cols],
-                    rhs=x_codes[(j, operand)][:].bitcast(FP8X4),
-                    rhs_scale=x_planes[(j, operand)][:],
+                    rhs=x_codes[(j, operands[k_pass])][:].bitcast(FP8X4),
+                    rhs_scale=x_planes[(j, operands[k_pass])][:],
                     start=(k_pass == 0),
                     stop=(k_pass == K_PASSES - 1),
                 )
+
+            if between_passes is None:
+                for f in range(F_TILES):
+                    for k_pass in range(K_PASSES):
+                        one_pass(f, k_pass)
+            else:
+                for f in range(F_TILES):
+                    one_pass(f, 0)
+                between_passes()
+                for f in range(F_TILES):
+                    one_pass(f, 1)
             return banks
 
         def activate(name, banks, bufs=1):
@@ -300,198 +243,108 @@ def tile_customlstmcell_kernel(
         def gate(j, name, bufs=1):
             return activate(name, multiply(j, name), bufs)
 
-        def combine(target, other, op, kind, engine=nc.vector):
-            step = OPT["wide"][kind]
-            for f in range(0, F_TILES, step):
-                engine.tensor_tensor(
-                    out=target[:, f : f + step, :], in0=target[:, f : f + step, :], in1=other[:, f : f + step, :], op=op
-                )
+        def combine(target, other, op):
+            for f in range(F_TILES):
+                nc.vector.tensor_tensor(out=target[:, f, :], in0=target[:, f, :], in1=other[:, f, :], op=op)
 
-        def turn_back(source, block, spare=False):
-            if spare:
-                bank = z_banks.tile([P, H], F32, tag="z", name="spare_bank")
+        def turn_back(block, pieces, from_z_banks=False):
+            if from_z_banks:
+                bank = z_banks.tile([P, H], F32, tag="z", name="bank")
             else:
                 bank = t_banks.tile([P, H], F32, tag="t", name="bank")
+            rows = slice(block * P, (block + 1) * P)
             for f in range(F_TILES):
-                nc.tensor.transpose(
-                    out=bank[:, f * P : (f + 1) * P],
-                    in_=source[:, f, block * P : (block + 1) * P],
-                    identity=identity[:],
-                )
+                for number, piece in enumerate(pieces):
+                    nc.tensor.matmul(
+                        out=bank[:, f * P : (f + 1) * P],
+                        lhsT=piece[:, f, rows],
+                        rhs=identity[:],
+                        is_transpose=True,
+                        start=(number == 0),
+                        stop=(number == len(pieces) - 1),
+                    )
             return bank
 
         def out_rows(dram, j, block):
-            if OPT["pairs"]:
-                first = j * CHUNK + (block // 2) * 2 * P
-                return dram[first : first + 2 * P, :].rearrange("(p e) k -> p e k", e=2)[:, block % 2, :]
             first = j * CHUNK + block * P
             return dram[first : first + P, :]
 
-        def out_pair(dram, j, half):
-            first = j * CHUNK + half * 2 * P
-            return dram[first : first + 2 * P, :].rearrange("(p e) k -> p e k", e=2)
-
-        kept = {}
-
-        def cell_state(j, keep, feed, blocks, c_tiles):
-            ahead = OPT["keep_ahead"] and j == N_CHUNKS - 1
-            keep_banks = {} if ahead and blocks == LATE else {block: turn_back(keep, block) for block in blocks}
-            feed_banks = {block: turn_back(feed, block) for block in blocks}
-            if ahead and blocks == EARLY:
-                for block in LATE:
-                    keep_banks[block] = turn_back(keep, block, spare=True)
+        def cell_state(j, keep, feed, blocks, kept, c_tiles, keep_ahead=()):
+            keep_banks = {block: turn_back(block, (keep,)) for block in blocks if block not in kept}
+            feed_banks = {block: turn_back(block, (feed,)) for block in blocks}
+            for block in keep_ahead:
+                keep_banks[block] = turn_back(block, (keep,), from_z_banks=True)
             for block in sorted(keep_banks):
-                kept[block] = rowwise.tile([P, H], F32, tag="kept", name="kept", bufs=4 if OPT["keep_ahead"] else 2)
+                kept[block] = rowwise.tile([P, H], F32, tag="kept", name="kept")
                 nc.vector.tensor_tensor(
                     out=kept[block][:], in0=keep_banks[block][:], in1=c_rows[j][:, block, :], op=MULT
                 )
-            c_pair = rowwise.tile([P, 2, H], F32, tag="c_new", name="c_pair", bufs=2)
-            together = OPT["pair_stores"] and not (j == N_CHUNKS - 1 and blocks == LATE)
             for block in blocks:
-                c_tile = c_pair[:, block % 2, :]
-                nc.vector.tensor_tensor(out=c_tile, in0=feed_banks[block][:], in1=kept[block][:], op=ADD)
-                if not together:
-                    nc.sync.dma_start(out=out_rows(c_new, j, block), in_=c_tile)
+                c_tile = rowwise.tile([P, H], F32, tag="c_new")
+                nc.vector.tensor_tensor(out=c_tile[:], in0=feed_banks[block][:], in1=kept[block][:], op=ADD)
+                nc.sync.dma_start(out=out_rows(c_new, j, block), in_=c_tile[:])
                 c_tiles[block] = c_tile
-            if together:
-                nc.sync.dma_start(out=out_pair(c_new, j, blocks[0] // 2), in_=c_pair[:])
 
         def tanh_of_cell(blocks, c_tiles, tanh_tiles):
             for block in blocks:
                 tanh_c = rowwise.tile([P, H], F32, tag="tanh_c")
-                nc.scalar.activation(out=tanh_c[:], in_=c_tiles[block], func=TANH)
+                nc.scalar.activation(out=tanh_c[:], in_=c_tiles[block][:], func=TANH)
                 tanh_tiles[block] = tanh_c
 
-        def hidden_state(j, open_gate, tanh_tiles):
-            last = j == N_CHUNKS - 1
-            sources = open_gate if isinstance(open_gate, tuple) else (open_gate,)
-            if last and OPT["tail_z"]:
-                banks = [z_banks.tile([P, H], F32, tag="z", name="open_bank") for block in range(BLOCKS)]
-            else:
-                banks = [t_banks.tile([P, H], F32, tag="t", name="open_bank") for block in range(BLOCKS)]
-            if last and OPT["tail_f_major"]:
-                order = [(block, f) for f in range(F_TILES) for block in range(BLOCKS)]
-            else:
-                order = [(block, f) for block in range(BLOCKS) for f in range(F_TILES)]
-            two_banks = last and OPT["tail_two_banks"]
-            if two_banks:
-                extra = z_banks.tile([P, H], F32, tag="z", name="extra_bank")
-            for block, f in order:
-                summed = sources if f in OPT["open_pe_tiles"] else sources[:1]
-                in_extra = two_banks and block == BLOCKS - 1 and f >= F_TILES // 2
-                for number, source in enumerate(summed):
-                    nc.tensor.matmul(
-                        out=extra[:, (f - F_TILES // 2) * P : (f - F_TILES // 2 + 1) * P] if in_extra else banks[block][:, f * P : (f + 1) * P],
-                        lhsT=source[:, f, block * P : (block + 1) * P],
-                        rhs=identity[:],
-                        is_transpose=True,
-                        start=(number == 0),
-                        stop=(number == len(summed) - 1),
-                    )
+        def hidden_state(j, open_pieces, tanh_tiles):
+            banks = [turn_back(block, open_pieces) for block in range(BLOCKS)]
             for block in range(BLOCKS):
-                if block % 2 == 0:
-                    h_pair = rowwise.tile([P, 2, H], F32, tag="h_new", name="h_pair", bufs=2)
-                h_tile = h_pair[:, block % 2, :]
-                together = OPT["pair_stores"] and not last
-                pieces = OPT["tail_split"] if last and block == BLOCKS - 1 else 1
-                for piece in range(pieces):
-                    cols = slice(piece * H // pieces, (piece + 1) * H // pieces)
-                    nc.vector.tensor_tensor(
-                        out=h_tile[:, cols],
-                        in0=extra[:, 0 : H // 2] if two_banks and pieces == 2 and piece == 1 else banks[block][:, cols],
-                        in1=tanh_tiles[block][:, cols], op=MULT,
-                    )
-                    if not together:
-                        nc.sync.dma_start(out=out_rows(h_new, j, block)[:, cols], in_=h_tile[:, cols])
-                if together and block % 2 == 1:
-                    nc.sync.dma_start(out=out_pair(h_new, j, block // 2), in_=h_pair[:])
+                h_tile = rowwise.tile([P, H], F32, tag="h_new")
+                nc.vector.tensor_tensor(out=h_tile[:], in0=banks[block][:], in1=tanh_tiles[block][:], op=MULT)
+                nc.sync.dma_start(out=out_rows(h_new, j, block), in_=h_tile[:])
 
-        def finish_chunk(j, open_gate, c_tiles, tanh_tiles):
+        def finish_chunk(j, open_pieces, c_tiles, tanh_tiles):
             tanh_of_cell(LATE, c_tiles, tanh_tiles)
-            hidden_state(j, open_gate, tanh_tiles)
+            hidden_state(j, open_pieces, tanh_tiles)
 
-        transpose_x(0, "h_light", OPT_ENGINES[OPT["head_copies"][0]], OPT["dummies"][1], OPT["head_halves"])
-        if not OPT["head_halves"]:
-            quantise_x(0, "h_light")
-        transpose_x(0, "y", OPT_ENGINES[OPT["head_copies"][1]], OPT["dummies"][1], OPT["head_halves"])
-        if not OPT["bias0_mid"]:
-            transpose_biases(0)
-        keep_warm(OPT["dummies"][2])
-        if not OPT["head_halves"]:
-            quantise_x(0, "y")
-        sort_x(0, "h_temp")
-
-        waiting = []
-
-        def prepare(behind):
-            items = OPT["prep"].get(behind, ())
-            for item in items:
-                if item.startswith("bias"):
-                    transpose_biases(int(item[-1]))
-                else:
-                    transpose_x(1, item)
-            if OPT["defer_q"]:
-                for item in waiting:
-                    quantise_x(1, item)
-                waiting.clear()
-            for item in items:
-                if not item.startswith("bias"):
-                    if OPT["defer_q"]:
-                        waiting.append(item)
-                    else:
-                        quantise_x(1, item)
+        transpose_x(0, "h_light")
+        quantise_x(0, "h_light")
+        transpose_x(0, "y", copy_engines=(nc.scalar, nc.scalar))
+        quantise_x(0, "y")
 
         for j in range(N_CHUNKS):
-            banks = multiply(
-                j, "i1", pass_major=(j == 0 and OPT["pass_major_first"]),
-                between=(lambda: transpose_biases(0)) if j == 0 and OPT["bias0_mid"] else None,
-            )
+            if j == 0:
+                banks = multiply(0, "i1", between_passes=lambda: transpose_biases(0))
+            else:
+                banks = multiply(j, "i1")
             feed = activate("i1", banks, bufs=2)
             if j == 0:
-                transpose_x(0, "h_temp")
-                prepare("i1")
-                quantise_x(0, "h_temp")
-                sort_x(1, "h_light")
-            combine(feed, gate(j, "c1"), MULT, "mult")
+                prepare_x(0, "h_temp")
+            combine(feed, gate(j, "c1"), MULT)
             if j == 0:
-                prepare("c1")
-                sort_x(1, "y")
+                prepare_x(1, "h_light")
             else:
                 finish_chunk(*unfinished)
 
             feed_2 = gate(j, "i2")
             if j == 0:
-                prepare("i2")
-                sort_x(1, "h_temp")
-            combine(feed_2, gate(j, "c2"), MULT, "mult")
+                prepare_x(1, "y")
+            combine(feed_2, gate(j, "c2"), MULT)
             if j == 0:
-                prepare("c2")
-            combine(feed, feed_2, ADD, "feed")
-            if j == 0:
-                prepare("feed")
+                transpose_x(1, "h_temp")
+                transpose_biases(1)
+                quantise_x(1, "h_temp")
+            combine(feed, feed_2, ADD)
 
             keep = gate(j, "f1", bufs=2)
-            if j == 0:
-                prepare("f1")
-            combine(keep, gate(j, "f2"), ADD, "keep")
-            if j == 0:
-                prepare("f2")
+            combine(keep, gate(j, "f2"), ADD)
 
-            open_gate = gate(j, "o1", bufs=2)
-            c_tiles, tanh_tiles = {}, {}
-            cell_state(j, keep, feed, EARLY, c_tiles)
-            if j in OPT["open_on_pe"]:
-                second = gate(j, "o2")
-                for f in range(F_TILES):
-                    if f not in OPT["open_pe_tiles"]:
-                        nc.vector.tensor_tensor(
-                            out=open_gate[:, f, :], in0=open_gate[:, f, :], in1=second[:, f, :], op=ADD
-                        )
-                open_gate = (open_gate, second)
+            open_1 = gate(j, "o1", bufs=2)
+            kept, c_tiles, tanh_tiles = {}, {}, {}
+            cell_state(j, keep, feed, EARLY, kept, c_tiles, keep_ahead=LATE if j == LAST else ())
+            open_2 = gate(j, "o2")
+            if j == LAST:
+                open_pieces = (open_1, open_2)
             else:
-                combine(open_gate, gate(j, "o2"), ADD, "open", nc.gpsimd if j in OPT["open_on_pool"] else nc.vector)
+                combine(open_1, open_2, ADD)
+                open_pieces = (open_1,)
             tanh_of_cell(EARLY, c_tiles, tanh_tiles)
-            cell_state(j, keep, feed, LATE, c_tiles)
-            unfinished = (j, open_gate, c_tiles, tanh_tiles)
+            cell_state(j, keep, feed, LATE, kept, c_tiles)
+            unfinished = (j, open_pieces, c_tiles, tanh_tiles)
 
         finish_chunk(*unfinished)

@@ -70,7 +70,7 @@ def tile_customlstmcell_kernel(
         t_banks = ctx.enter_context(tc.psum_pool(name="t_banks", bufs=4))
         ctx.enter_context(tc.manual_schedule())
 
-        w_planes = resident.tile([P, len(gates), H], U8, name="w_planes", align_bytes=64)
+        w_planes = resident.tile([P, len(gates), H], U8, name="w_planes", align_bytes=256)
         nc.vector.memset(w_planes[:, 0, :].bitcast(I32), 0)
 
         bias_rows = [resident.tile([P, P], BF16, name="bias_rows_%d" % group) for group in range(bias_groups)]
@@ -116,7 +116,7 @@ def tile_customlstmcell_kernel(
 
         def load_words(name, k_passes):
             if name not in w_words:
-                w_words[name] = resident.tile([P, K_PASSES, H], U32, name="words_%s" % name, align_bytes=64)
+                w_words[name] = resident.tile([P, K_PASSES, H], U32, name="words_%s" % name, align_bytes=256)
             nc.sync.dma_start(
                 out=w_words[name][:, k_passes, :].bitcast(I32),
                 in_=gates[gate_number[name]][1][k_passes].rearrange("g p n t -> p g (n t)").bitcast(I32),
@@ -157,7 +157,7 @@ def tile_customlstmcell_kernel(
         x_grouped, x_codes, x_planes = {}, {}, {}
 
         def transpose_x(j, operand, copy_engines=(nc.vector, nc.scalar)):
-            grouped = stage.tile([P, 4 * CHUNK], BF16, tag="grouped", align_bytes=64)
+            grouped = stage.tile([P, 4 * CHUNK], BF16, tag="grouped", align_bytes=256)
             grouped_words = grouped[:].bitcast(F32).rearrange("p (r u) -> p r u", u=2)
             for bank in range(CHUNK // BANK_ROWS):
                 turned = t_banks.tile([P, 2, BANK_ROWS], F32, tag="t")
@@ -178,8 +178,8 @@ def tile_customlstmcell_kernel(
             x_grouped[(j, operand)] = grouped
 
         def quantise_x(j, operand):
-            codes = resident.tile([P, CHUNK], U32, name="codes_%s_%d" % (operand, j), align_bytes=64)
-            plane = resident.tile([P, CHUNK], U8, name="plane_%s_%d" % (operand, j), align_bytes=64)
+            codes = resident.tile([P, CHUNK], U32, name="codes_%s_%d" % (operand, j), align_bytes=256)
+            plane = resident.tile([P, CHUNK], U8, name="plane_%s_%d" % (operand, j), align_bytes=256)
             nc.vector.quantize_mx(
                 out=codes[:].bitcast(FP8X4), scales=plane[:], in_=x_grouped[(j, operand)][:]
             )

@@ -27,6 +27,7 @@ EARLY, LATE = (0, 1), (2, 3)
 BANK = 512
 BANK_ROWS = BANK // 2
 GATES_IN_BIAS_GROUP = 4
+WARM_UP_MATMULS = 4
 
 FLOPS = 2 * ROWS * (2 * H) * (8 * H)
 BYTES = 4 * ROWS * H * 2 + 8 * (2 * H * H + 2 * 16 * H + H * 2) + 2 * ROWS * H * 4
@@ -72,6 +73,12 @@ def tile_customlstmcell_kernel(
 
         w_planes = resident.tile([P, len(gates), H], U8, name="w_planes", align_bytes=256)
         nc.vector.memset(w_planes[:, 0, :].bitcast(I32), 0)
+
+        zeros = resident.tile([P, CHUNK], BF16, name="zeros")
+        nc.vector.memset(zeros[:].bitcast(I32), 0)
+        for number in range(WARM_UP_MATMULS):
+            unread = z_banks.tile([P, CHUNK], F32, tag="z", name="unread")
+            nc.tensor.matmul(out=unread[:], lhsT=zeros[:, 0:P], rhs=zeros[:], start=True, stop=True)
 
         bias_rows = [resident.tile([P, P], BF16, name="bias_rows_%d" % group) for group in range(bias_groups)]
         for group in range(bias_groups):
@@ -156,7 +163,7 @@ def tile_customlstmcell_kernel(
 
         x_grouped, x_codes, x_planes = {}, {}, {}
 
-        def transpose_x(j, operand, copy_engines=(nc.vector, nc.scalar)):
+        def transpose_x(j, operand, copy_engines=(nc.vector, nc.scalar), quantise_each_bank=False):
             grouped = stage.tile([P, 4 * CHUNK], BF16, tag="grouped", align_bytes=256)
             grouped_words = grouped[:].bitcast(F32).rearrange("p (r u) -> p r u", u=2)
             for bank in range(CHUNK // BANK_ROWS):
@@ -175,15 +182,23 @@ def tile_customlstmcell_kernel(
                     out=grouped_words[:, bank * BANK_ROWS : (bank + 1) * BANK_ROWS, :],
                     in_=turned[:].rearrange("p u r -> p r u"),
                 )
-            x_grouped[(j, operand)] = grouped
+                x_grouped[(j, operand)] = grouped
+                if quantise_each_bank:
+                    quantise_x(j, operand, slice(bank * BANK_ROWS, (bank + 1) * BANK_ROWS))
 
-        def quantise_x(j, operand):
-            codes = resident.tile([P, CHUNK], U32, name="codes_%s_%d" % (operand, j), align_bytes=256)
-            plane = resident.tile([P, CHUNK], U8, name="plane_%s_%d" % (operand, j), align_bytes=256)
+        def quantise_x(j, operand, rows=slice(0, CHUNK)):
+            if (j, operand) not in x_codes:
+                x_codes[(j, operand)] = resident.tile(
+                    [P, CHUNK], U32, name="codes_%s_%d" % (operand, j), align_bytes=256
+                )
+                x_planes[(j, operand)] = resident.tile(
+                    [P, CHUNK], U8, name="plane_%s_%d" % (operand, j), align_bytes=256
+                )
             nc.vector.quantize_mx(
-                out=codes[:].bitcast(FP8X4), scales=plane[:], in_=x_grouped[(j, operand)][:]
+                out=x_codes[(j, operand)][:, rows].bitcast(FP8X4),
+                scales=x_planes[(j, operand)][:, rows],
+                in_=x_grouped[(j, operand)][:, 4 * rows.start : 4 * rows.stop],
             )
-            x_codes[(j, operand)], x_planes[(j, operand)] = codes, plane
 
         def prepare_x(j, operand):
             transpose_x(j, operand)
@@ -302,10 +317,8 @@ def tile_customlstmcell_kernel(
             tanh_of_cell(LATE, c_tiles, tanh_tiles)
             hidden_state(j, open_pieces, tanh_tiles)
 
-        transpose_x(0, "h_light")
-        quantise_x(0, "h_light")
-        transpose_x(0, "y", copy_engines=(nc.scalar, nc.scalar))
-        quantise_x(0, "y")
+        transpose_x(0, "h_light", quantise_each_bank=True)
+        transpose_x(0, "y", copy_engines=(nc.scalar, nc.scalar), quantise_each_bank=True)
 
         for j in range(N_CHUNKS):
             if j == 0:

@@ -76,9 +76,13 @@ def tile_customlstmcell_kernel(
 
         zeros = resident.tile([P, CHUNK], BF16, name="zeros")
         nc.vector.memset(zeros[:].bitcast(I32), 0)
-        for number in range(WARM_UP_MATMULS):
+
+        def keep_warm():
             unread = z_banks.tile([P, CHUNK], F32, tag="z", name="unread")
             nc.tensor.matmul(out=unread[:], lhsT=zeros[:, 0:P], rhs=zeros[:], start=True, stop=True)
+
+        for number in range(WARM_UP_MATMULS):
+            keep_warm()
 
         bias_rows = [resident.tile([P, P], BF16, name="bias_rows_%d" % group) for group in range(bias_groups)]
         for group in range(bias_groups):
@@ -163,7 +167,7 @@ def tile_customlstmcell_kernel(
 
         x_grouped, x_codes, x_planes = {}, {}, {}
 
-        def transpose_x(j, operand, copy_engines=(nc.vector, nc.scalar), quantise_each_bank=False):
+        def transpose_x(j, operand, copy_engines=(nc.vector, nc.scalar), quantise_each_bank=False, warm_behind=()):
             grouped = stage.tile([P, 4 * CHUNK], BF16, tag="grouped", align_bytes=256)
             grouped_words = grouped[:].bitcast(F32).rearrange("p (r u) -> p r u", u=2)
             for bank in range(CHUNK // BANK_ROWS):
@@ -185,6 +189,8 @@ def tile_customlstmcell_kernel(
                 x_grouped[(j, operand)] = grouped
                 if quantise_each_bank:
                     quantise_x(j, operand, slice(bank * BANK_ROWS, (bank + 1) * BANK_ROWS))
+                if (operand, bank) in warm_behind:
+                    keep_warm()
 
         def quantise_x(j, operand, rows=slice(0, CHUNK)):
             if (j, operand) not in x_codes:
@@ -317,8 +323,9 @@ def tile_customlstmcell_kernel(
             tanh_of_cell(LATE, c_tiles, tanh_tiles)
             hidden_state(j, open_pieces, tanh_tiles)
 
-        transpose_x(0, "h_light", quantise_each_bank=True)
-        transpose_x(0, "y", copy_engines=(nc.scalar, nc.scalar), quantise_each_bank=True)
+        behind = (("h_light", 1), ("y", 0))
+        transpose_x(0, "h_light", quantise_each_bank=True, warm_behind=behind)
+        transpose_x(0, "y", copy_engines=(nc.scalar, nc.scalar), quantise_each_bank=True, warm_behind=behind)
 
         for j in range(N_CHUNKS):
             if j == 0:

@@ -165,7 +165,17 @@ def tile_customlstmcell_kernel(
         load_weight("o2")
         load_c(1)
 
-        x_grouped, x_codes, x_planes = {}, {}, {}
+        x_grouped, x_codes, x_planes, x_sorted = {}, {}, {}, {}
+
+        def sort_words(j, operand):
+            ordered = resident.tile([P, BLOCKS, 2, P], F32, name="sorted_%s_%d" % (operand, j))
+            nc.vector.tensor_copy(
+                out=ordered[:],
+                in_=x_raw[(j, operand)][:].rearrange("p b k -> p (b k)").bitcast(F32).rearrange(
+                    "p (b q u) -> p b u q", b=BLOCKS, u=2
+                ),
+            )
+            x_sorted[(j, operand)] = ordered
 
         def transpose_x(j, operand, copy_engines=(nc.vector, nc.scalar), quantise_each_bank=False, warm_behind=()):
             grouped = stage.tile([P, 4 * CHUNK], BF16, tag="grouped", align_bytes=256)
@@ -173,11 +183,16 @@ def tile_customlstmcell_kernel(
             for bank in range(CHUNK // BANK_ROWS):
                 turned = t_banks.tile([P, 2, BANK_ROWS], F32, tag="t")
                 for half in range(BANK_ROWS // P):
-                    words = x_raw[(j, operand)][:, bank * (BANK_ROWS // P) + half, :].bitcast(F32)
+                    block = bank * (BANK_ROWS // P) + half
+                    words = x_raw[(j, operand)][:, block, :].bitcast(F32)
                     for u in range(2):
+                        if (j, operand) in x_sorted:
+                            picked = x_sorted[(j, operand)][:, block, u, :]
+                        else:
+                            picked = words[:, u : H // 2 : 2]
                         nc.tensor.transpose(
                             out=turned[:, u, half * P : (half + 1) * P],
-                            in_=words[:, u : H // 2 : 2],
+                            in_=picked,
                             identity=identity[:],
                         )
                 engine = copy_engines[bank]
@@ -264,8 +279,10 @@ def tile_customlstmcell_kernel(
         def gate(j, name, bufs=1):
             return activate(name, multiply(j, name), bufs)
 
-        def combine(target, other, op):
+        def combine(target, other, op, ahead_of_last=None):
             for f in range(F_TILES):
+                if ahead_of_last is not None and f == F_TILES - 1:
+                    ahead_of_last()
                 nc.vector.tensor_tensor(out=target[:, f, :], in0=target[:, f, :], in1=other[:, f, :], op=op)
 
         def turn_back(block, pieces, from_z_banks=False):
@@ -333,22 +350,28 @@ def tile_customlstmcell_kernel(
             else:
                 banks = multiply(j, "i1")
             feed = activate("i1", banks, bufs=2)
+            if j == 1:
+                quantise_x(1, "h_temp")
             if j == 0:
-                prepare_x(0, "h_temp")
-            combine(feed, gate(j, "c1"), MULT)
+                transpose_x(0, "h_temp")
+                sort_words(1, "h_light")
+                quantise_x(0, "h_temp")
+            combine(feed, gate(j, "c1"), MULT, (lambda: sort_words(1, "y")) if j == 0 else None)
             if j == 0:
-                prepare_x(1, "h_light")
+                transpose_x(1, "h_light")
+                quantise_x(1, "h_light")
             else:
                 finish_chunk(*unfinished)
 
             feed_2 = gate(j, "i2")
             if j == 0:
-                prepare_x(1, "y")
+                transpose_x(1, "y")
+                sort_words(1, "h_temp")
+                quantise_x(1, "y")
             combine(feed_2, gate(j, "c2"), MULT)
             if j == 0:
                 transpose_x(1, "h_temp")
                 transpose_biases(1)
-                quantise_x(1, "h_temp")
             combine(feed, feed_2, ADD)
 
             keep = gate(j, "f1", bufs=2)

@@ -28,6 +28,7 @@ BANK = 512
 BANK_ROWS = BANK // 2
 GATES_IN_BIAS_GROUP = 4
 WARM_UP_MATMULS = 4
+PLANE_SHIFT = 128
 
 FLOPS = 2 * ROWS * (2 * H) * (8 * H)
 BYTES = 4 * ROWS * H * 2 + 8 * (2 * H * H + 2 * 16 * H + H * 2) + 2 * ROWS * H * 4
@@ -213,11 +214,11 @@ def tile_customlstmcell_kernel(
                     [P, CHUNK], U32, name="codes_%s_%d" % (operand, j), align_bytes=256
                 )
                 x_planes[(j, operand)] = resident.tile(
-                    [P, CHUNK], U8, name="plane_%s_%d" % (operand, j), align_bytes=256
+                    [P, PLANE_SHIFT + CHUNK], U8, name="plane_%s_%d" % (operand, j), align_bytes=256
                 )
             nc.vector.quantize_mx(
                 out=x_codes[(j, operand)][:, rows].bitcast(FP8X4),
-                scales=x_planes[(j, operand)][:, rows],
+                scales=x_planes[(j, operand)][:, PLANE_SHIFT + rows.start : PLANE_SHIFT + rows.stop],
                 in_=x_grouped[(j, operand)][:, 4 * rows.start : 4 * rows.stop],
             )
 
@@ -248,7 +249,7 @@ def tile_customlstmcell_kernel(
                     lhsT=w_words[name][:, k_pass, cols].bitcast(FP8X4),
                     lhsT_scale=w_planes[4 * k_pass : P, number, cols],
                     rhs=x_codes[(j, operands[k_pass])][:].bitcast(FP8X4),
-                    rhs_scale=x_planes[(j, operands[k_pass])][:],
+                    rhs_scale=x_planes[(j, operands[k_pass])][:, PLANE_SHIFT:],
                     start=(k_pass == 0),
                     stop=(k_pass == K_PASSES - 1),
                 )

from contextlib import ExitStack

import concourse.mybir as mybir
from concourse.masks import make_identity

F32 = mybir.dt.float32
BF16 = mybir.dt.bfloat16
I32 = mybir.dt.int32
U32 = mybir.dt.uint32
U8 = mybir.dt.uint8
FP8X4 = mybir.dt.float8_e4m3fn_x4
SIGMOID = mybir.ActivationFunctionType.Sigmoid
TANH = mybir.ActivationFunctionType.Tanh
ADD = mybir.AluOpType.add
MULT = mybir.AluOpType.mult

P = 128
ROWS = 1024
H = 512
K_PASSES = 2
F_TILES = H // P
CHUNK = 512
N_CHUNKS = ROWS // CHUNK
LAST = N_CHUNKS - 1
BLOCKS = CHUNK // P
EARLY, LATE = (0, 1), (2, 3)
BANK = 512
BANK_ROWS = BANK // 2
GATES_IN_BIAS_GROUP = 4
WARM_UP_MATMULS = 4
PLANE_SHIFT = 128

FLOPS = 2 * ROWS * (2 * H) * (8 * H)
BYTES = 4 * ROWS * H * 2 + 8 * (2 * H * H + 2 * 16 * H + H * 2) + 2 * ROWS * H * 4


def tile_customlstmcell_kernel(
    tc, y, h_light, c_light, h_temp, c_temp,
    w_f_light_words, w_f_light_scales, b_f_light,
    w_i_light_words, w_i_light_scales, b_i_light,
    w_c_light_words, w_c_light_scales, b_c_light,
    w_o_light_words, w_o_light_scales, b_o_light,
    w_f_light_temp_words, w_f_light_temp_scales, b_f_light_temp,
    w_i_light_temp_words, w_i_light_temp_scales, b_i_light_temp,
    w_c_light_temp_words, w_c_light_temp_scales, b_c_light_temp,
    w_o_light_temp_words, w_o_light_temp_scales, b_o_light_temp,
    out_0, out_1,
):
    nc = tc.nc
    h_new, c_new = out_0, out_1
    x_dram = {"h_light": h_light, "h_temp": h_temp, "y": y}

    gates = (
        ("i1", w_i_light_words, w_i_light_scales, b_i_light, "h_light", SIGMOID),
        ("c1", w_c_light_words, w_c_light_scales, b_c_light, "h_light", TANH),
        ("i2", w_i_light_temp_words, w_i_light_temp_scales, b_i_light_temp, "h_temp", SIGMOID),
        ("c2", w_c_light_temp_words, w_c_light_temp_scales, b_c_light_temp, "h_temp", TANH),
        ("f1", w_f_light_words, w_f_light_scales, b_f_light, "h_light", SIGMOID),
        ("f2", w_f_light_temp_words, w_f_light_temp_scales, b_f_light_temp, "h_temp", SIGMOID),
        ("o1", w_o_light_words, w_o_light_scales, b_o_light, "h_light", SIGMOID),
        ("o2", w_o_light_temp_words, w_o_light_temp_scales, b_o_light_temp, "h_temp", SIGMOID),
    )
    gate_number = {gate[0]: number for number, gate in enumerate(gates)}
    bias_groups = len(gates) // GATES_IN_BIAS_GROUP

    with ExitStack() as ctx:
        resident = ctx.enter_context(tc.tile_pool(name="resident", bufs=1))
        stage = ctx.enter_context(tc.tile_pool(name="stage", bufs=3))
        acts = ctx.enter_context(tc.tile_pool(name="acts", bufs=1))
        rowwise = ctx.enter_context(tc.tile_pool(name="rowwise", bufs=4))
        z_banks = ctx.enter_context(tc.psum_pool(name="z_banks", bufs=4))
        t_banks = ctx.enter_context(tc.psum_pool(name="t_banks", bufs=4))
        ctx.enter_context(tc.manual_schedule())

        w_planes = resident.tile([P, len(gates), H], U8, name="w_planes", align_bytes=256)
        nc.vector.memset(w_planes[:, 0, :].bitcast(I32), 0)

        zeros = resident.tile([P, CHUNK], BF16, name="zeros")
        nc.vector.memset(zeros[:].bitcast(I32), 0)

        def keep_warm():
            unread = z_banks.tile([P, CHUNK], F32, tag="z", name="unread")
            nc.tensor.matmul(out=unread[:], lhsT=zeros[:, 0:P], rhs=zeros[:], start=True, stop=True)

        for number in range(WARM_UP_MATMULS):
            keep_warm()

        bias_rows = [resident.tile([P, P], BF16, name="bias_rows_%d" % group) for group in range(bias_groups)]
        for group in range(bias_groups):
            nc.vector.memset(bias_rows[group][:], 0.0)

        warm = resident.tile([P, 1], F32, name="warm")
        nc.vector.memset(warm[:], 0.0)
        nc.scalar.activation(out=warm[:], in_=warm[:], func=SIGMOID)

        identity = resident.tile([P, P], F32, name="identity")
        make_identity(nc, identity[:])

        nc.vector.memset(w_planes[:, 1:, :].bitcast(I32), 0)

        x_raw, c_rows, w_words = {}, {}, {}

        def load_rows(dram, j, name, pieces=1):
            rows = resident.tile([P, BLOCKS, H], BF16, name="%s_%d" % (name, j))
            blocks = BLOCKS // pieces
            for piece in range(pieces):
                first = j * CHUNK + piece * blocks * P
                nc.sync.dma_start(
                    out=rows[:, piece * blocks : (piece + 1) * blocks, :],
                    in_=dram[first : first + blocks * P, :].rearrange("(b p) k -> p b k", p=P),
                )
            return rows

        def load_x(j, operand, pieces=1):
            x_raw[(j, operand)] = load_rows(x_dram[operand], j, operand, pieces)

        def load_c(j):
            c_rows[j] = load_rows(c_light, j, "c_light")

        def load_scales(name):
            number = gate_number[name]
            for quadrant in range(4):
                first = 32 * quadrant
                nc.sync.dma_start(
                    out=w_planes[first : first + 4 * K_PASSES, number, :].bitcast(I32),
                    in_=gates[number][2][:, 4 * quadrant : 4 * quadrant + 4, :].bitcast(I32),
                )

        def load_words(name, k_passes):
            if name not in w_words:
                w_words[name] = resident.tile([P, K_PASSES, H], U32, name="words_%s" % name, align_bytes=256)
            nc.sync.dma_start(
                out=w_words[name][:, k_passes, :].bitcast(I32),
                in_=gates[gate_number[name]][1][k_passes].rearrange("g p n t -> p g (n t)").bitcast(I32),
            )

        def load_weight(name):
            load_scales(name)
            load_words(name, slice(0, K_PASSES))

        def load_biases(group):
            for number in range(group * GATES_IN_BIAS_GROUP, (group + 1) * GATES_IN_BIAS_GROUP):
                nc.sync.dma_start(
                    out=bias_rows[group][F_TILES * number : F_TILES * (number + 1), :],
                    in_=gates[number][3].rearrange("(f c) -> f c", c=P),
                )

        load_x(0, "h_light", pieces=2)
        load_scales("i1")
        load_x(0, "y", pieces=2)
        load_words("i1", slice(0, 1))
        load_biases(0)
        load_words("i1", slice(1, 2))
        load_x(0, "h_temp")
        load_weight("c1")
        load_x(1, "h_light")
        load_weight("i2")
        load_x(1, "y")
        load_weight("c2")
        load_biases(1)
        load_x(1, "h_temp")
        load_weight("f1")
        load_weight("f2")
        load_weight("o1")
        load_c(0)
        load_weight("o2")
        load_c(1)

        x_grouped, x_codes, x_planes, x_sorted = {}, {}, {}, {}

        def sort_words(j, operand):
            ordered = resident.tile([P, BLOCKS, 2, P], F32, name="sorted_%s_%d" % (operand, j))
            nc.vector.tensor_copy(
                out=ordered[:],
                in_=x_raw[(j, operand)][:].rearrange("p b k -> p (b k)").bitcast(F32).rearrange(
                    "p (b q u) -> p b u q", b=BLOCKS, u=2
                ),
            )
            x_sorted[(j, operand)] = ordered

        def transpose_x(j, operand, copy_engines=(nc.vector, nc.scalar), quantise_each_bank=False, warm_behind=()):
            grouped = stage.tile([P, 4 * CHUNK], BF16, tag="grouped", align_bytes=256)
            grouped_words = grouped[:].bitcast(F32).rearrange("p (r u) -> p r u", u=2)
            for bank in range(CHUNK // BANK_ROWS):
                turned = t_banks.tile([P, 2, BANK_ROWS], F32, tag="t")
                for half in range(BANK_ROWS // P):
                    block = bank * (BANK_ROWS // P) + half
                    words = x_raw[(j, operand)][:, block, :].bitcast(F32)
                    for u in range(2):
                        if (j, operand) in x_sorted:
                            picked = x_sorted[(j, operand)][:, block, u, :]
                        else:
                            picked = words[:, u : H // 2 : 2]
                        nc.tensor.transpose(
                            out=turned[:, u, half * P : (half + 1) * P],
                            in_=picked,
                            identity=identity[:],
                        )
                engine = copy_engines[bank]
                copy_out = engine.tensor_copy if engine is nc.vector else engine.copy
                copy_out(
                    out=grouped_words[:, bank * BANK_ROWS : (bank + 1) * BANK_ROWS, :],
                    in_=turned[:].rearrange("p u r -> p r u"),
                )
                x_grouped[(j, operand)] = grouped
                if quantise_each_bank:
                    quantise_x(j, operand, slice(bank * BANK_ROWS, (bank + 1) * BANK_ROWS))
                if (operand, bank) in warm_behind:
                    keep_warm()

        def quantise_x(j, operand, rows=slice(0, CHUNK)):
            if (j, operand) not in x_codes:
                x_codes[(j, operand)] = resident.tile(
                    [P, CHUNK], U32, name="codes_%s_%d" % (operand, j), align_bytes=256
                )
                x_planes[(j, operand)] = resident.tile(
                    [P, PLANE_SHIFT + CHUNK], U8, name="plane_%s_%d" % (operand, j), align_bytes=256
                )
            nc.vector.quantize_mx(
                out=x_codes[(j, operand)][:, rows].bitcast(FP8X4),
                scales=x_planes[(j, operand)][:, PLANE_SHIFT + rows.start : PLANE_SHIFT + rows.stop],
                in_=x_grouped[(j, operand)][:, 4 * rows.start : 4 * rows.stop],
            )

        def prepare_x(j, operand):
            transpose_x(j, operand)
            quantise_x(j, operand)

        bias_cols = resident.tile([P, P], F32, name="bias_cols")

        def transpose_biases(group):
            bias_f32 = resident.tile([P, P], F32, name="bias_f32_%d" % group)
            nc.gpsimd.tensor_copy(out=bias_f32[:], in_=bias_rows[group][:])
            turned = t_banks.tile([P, P], F32, tag="t")
            nc.tensor.transpose(out=turned[:], in_=bias_f32[:], identity=identity[:])
            width = F_TILES * GATES_IN_BIAS_GROUP
            cols = slice(group * width, (group + 1) * width)
            nc.scalar.copy(out=bias_cols[:, cols], in_=turned[:, cols])

        def multiply(j, name, between_passes=None):
            number = gate_number[name]
            operands = (gates[number][4], "y")
            banks = [z_banks.tile([P, CHUNK], F32, tag="z", name="z") for f in range(F_TILES)]

            def one_pass(f, k_pass):
                cols = slice(f * P, (f + 1) * P)
                nc.tensor.matmul_mx(
                    out=banks[f][:],
                    lhsT=w_words[name][:, k_pass, cols].bitcast(FP8X4),
                    lhsT_scale=w_planes[4 * k_pass : P, number, cols],
                    rhs=x_codes[(j, operands[k_pass])][:].bitcast(FP8X4),
                    rhs_scale=x_planes[(j, operands[k_pass])][:, PLANE_SHIFT:],
                    start=(k_pass == 0),
                    stop=(k_pass == K_PASSES - 1),
                )

            if between_passes is None:
                for f in range(F_TILES):
                    for k_pass in range(K_PASSES):
                        one_pass(f, k_pass)
            else:
                for f in range(F_TILES):
                    one_pass(f, 0)
                between_passes()
                for f in range(F_TILES):
                    one_pass(f, 1)
            return banks

        def activate(name, banks, bufs=1):
            number = gate_number[name]
            result = acts.tile([P, F_TILES, CHUNK], F32, tag=name, name="act_" + name, bufs=bufs)
            for f in range(F_TILES):
                column = F_TILES * number + f
                nc.scalar.activation(
                    out=result[:, f, :], in_=banks[f][:], func=gates[number][5],
                    bias=bias_cols[:, column : column + 1],
                )
            return result

        def gate(j, name, bufs=1):
            return activate(name, multiply(j, name), bufs)

        def combine(target, other, op, ahead_of_last=None):
            for f in range(F_TILES):
                if ahead_of_last is not None and f == F_TILES - 1:
                    ahead_of_last()
                nc.vector.tensor_tensor(out=target[:, f, :], in0=target[:, f, :], in1=other[:, f, :], op=op)

        def turn_back(block, pieces, from_z_banks=False):
            if from_z_banks:
                bank = z_banks.tile([P, H], F32, tag="z", name="bank")
            else:
                bank = t_banks.tile([P, H], F32, tag="t", name="bank")
            rows = slice(block * P, (block + 1) * P)
            for f in range(F_TILES):
                for number, piece in enumerate(pieces):
                    nc.tensor.matmul(
                        out=bank[:, f * P : (f + 1) * P],
                        lhsT=piece[:, f, rows],
                        rhs=identity[:],
                        is_transpose=True,
                        start=(number == 0),
                        stop=(number == len(pieces) - 1),
                    )
            return bank

        def out_rows(dram, j, block):
            first = j * CHUNK + block * P
            return dram[first : first + P, :]

        def cell_state(j, keep, feed, blocks, kept, c_tiles, keep_ahead=()):
            keep_banks = {block: turn_back(block, (keep,)) for block in blocks if block not in kept}
            feed_banks = {block: turn_back(block, (feed,)) for block in blocks}
            for block in keep_ahead:
                keep_banks[block] = turn_back(block, (keep,), from_z_banks=True)
            for block in sorted(keep_banks):
                kept[block] = rowwise.tile([P, H], F32, tag="kept", name="kept")
                nc.vector.tensor_tensor(
                    out=kept[block][:], in0=keep_banks[block][:], in1=c_rows[j][:, block, :], op=MULT
                )
            for block in blocks:
                c_tile = rowwise.tile([P, H], F32, tag="c_new")
                nc.vector.tensor_tensor(out=c_tile[:], in0=feed_banks[block][:], in1=kept[block][:], op=ADD)
                nc.sync.dma_start(out=out_rows(c_new, j, block), in_=c_tile[:])
                c_tiles[block] = c_tile

        def tanh_of_cell(blocks, c_tiles, tanh_tiles):
            for block in blocks:
                tanh_c = rowwise.tile([P, H], F32, tag="tanh_c")
                nc.scalar.activation(out=tanh_c[:], in_=c_tiles[block][:], func=TANH)
                tanh_tiles[block] = tanh_c

        def hidden_state(j, open_pieces, tanh_tiles):
            banks = [turn_back(block, open_pieces) for block in range(BLOCKS)]
            for block in range(BLOCKS):
                h_tile = rowwise.tile([P, H], F32, tag="h_new")
                nc.vector.tensor_tensor(out=h_tile[:], in0=banks[block][:], in1=tanh_tiles[block][:], op=MULT)
                nc.sync.dma_start(out=out_rows(h_new, j, block), in_=h_tile[:])

        def finish_chunk(j, open_pieces, c_tiles, tanh_tiles):
            tanh_of_cell(LATE, c_tiles, tanh_tiles)
            hidden_state(j, open_pieces, tanh_tiles)

        behind = (("h_light", 1), ("y", 0))
        transpose_x(0, "h_light", quantise_each_bank=True, warm_behind=behind)
        transpose_x(0, "y", copy_engines=(nc.scalar, nc.scalar), quantise_each_bank=True, warm_behind=behind)

        for j in range(N_CHUNKS):
            if j == 0:
                banks = multiply(0, "i1", between_passes=lambda: transpose_biases(0))
            else:
                banks = multiply(j, "i1")
            feed = activate("i1", banks, bufs=2)
            if j == 1:
                quantise_x(1, "h_temp")
            if j == 0:
                transpose_x(0, "h_temp")
                sort_words(1, "h_light")
                quantise_x(0, "h_temp")
            combine(feed, gate(j, "c1"), MULT, (lambda: sort_words(1, "y")) if j == 0 else None)
            if j == 0:
                transpose_x(1, "h_light")
                quantise_x(1, "h_light")
            else:
                finish_chunk(*unfinished)

            feed_2 = gate(j, "i2")
            if j == 0:
                transpose_x(1, "y")
                sort_words(1, "h_temp")
                quantise_x(1, "y")
            combine(feed_2, gate(j, "c2"), MULT)
            if j == 0:
                transpose_x(1, "h_temp")
                transpose_biases(1)
            combine(feed, feed_2, ADD)

            keep = gate(j, "f1", bufs=2)
            combine(keep, gate(j, "f2"), ADD)

            open_1 = gate(j, "o1", bufs=2)
            kept, c_tiles, tanh_tiles = {}, {}, {}
            cell_state(j, keep, feed, EARLY, kept, c_tiles, keep_ahead=LATE if j == LAST else ())
            open_2 = gate(j, "o2")
            if j == LAST:
                open_pieces = (open_1, open_2)
            else:
                combine(open_1, open_2, ADD)
                open_pieces = (open_1,)
            tanh_of_cell(EARLY, c_tiles, tanh_tiles)
            cell_state(j, keep, feed, LATE, kept, c_tiles)
            unfinished = (j, open_pieces, c_tiles, tanh_tiles)

        finish_chunk(*unfinished)
